import numpy as np
import ml_dtypes


def mxq(x, axis, fmt="e4m3"):
    dtype, down = {"e4m3": (ml_dtypes.float8_e4m3fn, 7), "e5m2": (ml_dtypes.float8_e5m2, 14)}[fmt]
    v = np.moveaxis(np.asarray(x, np.float32).astype(ml_dtypes.bfloat16).astype(np.float64), axis, -1)
    blocks = v.reshape(v.shape[:-1] + (-1, 32))
    amax = np.abs(blocks).max(-1, keepdims=True)
    byte = np.maximum(np.where(amax > 0, np.frexp(amax)[1] - 1 + 127, 0) - down, 1)
    scale = np.exp2(byte - 127.0)
    codes = (blocks / scale).astype(np.float32).astype(dtype).astype(np.float64)
    return np.moveaxis((codes * scale).reshape(v.shape), -1, axis)


WIDE = False


def mx_kscale(k):
    if not WIDE:
        return np.ones(k)
    levels = np.array([10, -10, 5, -5, 0])
    if k % 512:
        return np.exp2(np.random.permutation(np.resize(levels, k // 32))).repeat(32)
    a = np.empty((k // 512, 16))
    for p in range(k // 512):
        a[p, :8] = np.random.permutation(np.resize(levels, 8))
        for g in range(8):
            far = levels[np.abs(levels - a[p, g]) >= 10]
            a[p, g + 8] = far[np.random.randint(len(far))]
    return np.exp2(a.ravel()).repeat(32)


BF16 = ml_dtypes.bfloat16


def bf(x):
    return np.asarray(x, np.float32).astype(BF16)


def f64(x):
    return np.asarray(x).astype(np.float64)


B, H, S, D = 4, 4, 1024, 128
TEMPERATURE = 8.0
QK = np.sqrt(1.5 * TEMPERATURE / np.sqrt(D))
VS = 3.0


def setup_inputs():
    t = mx_kscale(S)
    a = np.log2(t / t.min())
    q = np.random.standard_normal((B, H, S, D)) * QK
    k = np.random.standard_normal((B, H, S, D)) * QK
    v = np.random.standard_normal((B, H, S, D)) * VS
    q[..., 0] = TEMPERATURE
    k[..., 0] += a * np.log(2.0)
    v = v * (t.max() / t)[:, None]
    return {"q": bf(q), "k": bf(k), "v": bf(v),
            "mask": bf(np.random.randint(0, 2, (1, 1, S, S)))}


def reference(q, k, v, mask):
    s = f64(q) @ f64(k).transpose(0, 1, 3, 2) / TEMPERATURE * f64(mask)
    e = np.exp(s - s.max(-1, keepdims=True))
    return (mxq(e, 3, "e4m3") @ mxq(f64(v), 2, "e4m3")) / e.sum(-1, keepdims=True)

@@ -1,0 +1,306 @@
+from contextlib import ExitStack
+
+import concourse.mybir as mybir
+from concourse.masks import make_identity
+
+BF16 = mybir.dt.bfloat16
+F32 = mybir.dt.float32
+U32 = mybir.dt.uint32
+U8 = mybir.dt.uint8
+FP8X4 = mybir.dt.float8_e4m3fn_x4
+ALU = mybir.AluOpType
+ACT = mybir.ActivationFunctionType
+
+P = 128
+HEADS = 16
+S = 1024
+D = 128
+TEMPERATURE = 8.0
+Q_TILES = S // P
+UNITS = HEADS * Q_TILES
+GROUP = 4
+BANK = 512
+HALVES = S // BANK
+FIRST_HALF, LAST_HALF = 0, HALVES - 1
+PACK = 4
+K_PASS = P * PACK
+PASSES = S // K_PASS
+PAIR = 2
+WORD_BLOCKS = S // (PAIR * P)
+
+FLOPS = 2 * 2 * HEADS * S * S * D
+
+DETOURS = 2
+
+LOAD_LEAD = 16
+MASK_LEAD = 15
+Q_T_LEAD = 8
+K_T_LEAD = 4
+V_GROUP_LEAD = 10
+V_QUANT_LEAD = 2
+SCORE_LEAD = 2
+DETOUR_LEAD = 1
+MAX_LAG = 1
+EXP_LAG = 2
+E_T_LAG = 3
+PV_LAG = 7
+OUT_LAG = 8
+
+
+def tile_scaleddotproductattention_pa_kernel(tc, q, k, v, mask, out):
+    nc = tc.nc
+
+    q_heads = q.rearrange("b h (p t) d -> (b h) p t d", t=Q_TILES)
+    k_heads = k.rearrange("b h (t p) d -> (b h) p t d", p=P)
+    mask_tiles = mask.rearrange("a b (p t) k -> (a b) p t k", t=Q_TILES)
+    out_heads = out.rearrange("b h (p t) d -> (b h) p t d", t=Q_TILES)
+    v_heads = v.rearrange("b h (g p t) d -> (b h) p g t d", p=P, t=PACK)
+
+    with ExitStack() as ctx:
+        consts = ctx.enter_context(tc.tile_pool(name="consts", bufs=1))
+        heads = ctx.enter_context(tc.tile_pool(name="heads", bufs=3))
+        groups = ctx.enter_context(tc.tile_pool(name="groups", bufs=3))
+        units = ctx.enter_context(tc.tile_pool(name="units", bufs=3))
+        masked_pool = ctx.enter_context(tc.tile_pool(name="masked_pool", bufs=5))
+        score_psum = ctx.enter_context(tc.psum_pool(name="score_psum", bufs=3 * HALVES))
+        e_t_psum = ctx.enter_context(tc.psum_pool(name="e_t_psum", bufs=1))
+        shared_psum = ctx.enter_context(tc.psum_pool(name="shared_psum", bufs=1))
+
+        ident_bf16 = consts.tile([P, P], BF16)
+        make_identity(nc, ident_bf16[:])
+        ident_f32 = consts.tile([P, P], F32)
+        make_identity(nc, ident_f32[:])
+        mask_sb = consts.tile([P, Q_TILES, S], BF16)
+
+        q_rows, k_rows, v_rows, v_grouped = {}, {}, {}, {}
+        q_t, k_t, v_codes, v_scales = {}, {}, {}, {}
+        e_grouped, row_sums, pv = {}, {}, {}
+        scores, masked, neg_max, e_rows, e_t = {}, {}, {}, {}, {}
+
+        def load_head(head):
+            q_in = heads.tile([P, Q_TILES, D], BF16)
+            nc.sync.dma_start(out=q_in[:], in_=q_heads[head])
+            k_in = heads.tile([P, Q_TILES, D], BF16)
+            nc.sync.dma_start(out=k_in[:], in_=k_heads[head])
+            v_in = heads.tile([P, PASSES, PACK, D], BF16)
+            nc.sync.dma_start(out=v_in[:], in_=v_heads[head])
+            q_rows[head], k_rows[head], v_rows[head] = q_in, k_in, v_in
+
+        def transpose_rows(rows):
+            t_bank = shared_psum.tile([P, Q_TILES, P], BF16, tag="shared_bank")
+            for tile_index in range(Q_TILES):
+                nc.tensor.transpose(t_bank[:, tile_index, :], rows[:, tile_index, :], ident_bf16[:])
+            return t_bank
+
+        def transpose_q(head):
+            q_cols = heads.tile([P, Q_TILES, P], BF16)
+            nc.scalar.copy(out=q_cols[:], in_=transpose_rows(q_rows[head])[:])
+            q_t[head] = q_cols
+
+        def transpose_k(head):
+            k_cols = heads.tile([P, Q_TILES, P], BF16)
+            nc.scalar.copy(out=k_cols[:], in_=transpose_rows(k_rows[head])[:])
+            k_t[head] = k_cols
+
+        def regroup_v(head):
+            grouped = consts.tile([P, PASSES, D, PACK], BF16, align_bytes=64, name="v_grouped_keys")
+            nc.gpsimd.tensor_scalar(
+                out=grouped[:],
+                in0=v_rows[head][:].rearrange("p g t d -> p g d t"),
+                scalar1=1.0,
+                scalar2=0.0,
+                op0=ALU.mult,
+                op1=ALU.add,
+            )
+            v_grouped[head] = grouped
+
+        def quantise_v(head):
+            codes = heads.tile([P, PASSES, D], U32, align_bytes=64, name="v_code_words")
+            scale_plane = heads.tile([P, PASSES, D], U8, align_bytes=64, name="v_scale_plane")
+            nc.vector.quantize_mx(
+                out=codes[:].rearrange("p g d -> p (g d)").bitcast(FP8X4),
+                scales=scale_plane[:].rearrange("p g d -> p (g d)"),
+                in_=v_grouped[head][:].rearrange("p g d t -> p (g d t)"),
+            )
+            v_codes[head], v_scales[head] = codes, scale_plane
+
+        def takes_detour(unit):
+            return unit % GROUP < DETOURS
+
+        def multiply_q_k(unit):
+            head, tile_index = divmod(unit, Q_TILES)
+            masked_rows = masked_pool.tile([P, S], F32)
+            masked[unit] = masked_rows
+            for half in range(HALVES):
+                score_bank = score_psum.tile([P, BANK], F32)
+                key_tiles = slice(half * BANK // P, (half + 1) * BANK // P)
+                nc.tensor.matmul(
+                    out=score_bank[:],
+                    lhsT=q_t[head][:, tile_index, :],
+                    rhs=k_t[head][:, key_tiles, :].rearrange("d t p -> d (t p)"),
+                    start=True,
+                    stop=True,
+                )
+                scores[unit, half] = score_bank
+
+        def mask_scores(unit, half):
+            keys = slice(half * BANK, (half + 1) * BANK)
+            nc.vector.scalar_tensor_tensor(
+                out=masked[unit][:, keys],
+                in0=scores[unit, half][:],
+                scalar=1.0 / TEMPERATURE,
+                in1=mask_sb[:, unit % Q_TILES, keys],
+                op0=ALU.mult,
+                op1=ALU.mult,
+            )
+
+        def mask_scores_on_detour(unit, half):
+            keys = slice(half * BANK, (half + 1) * BANK)
+            scaled = units.tile([P, BANK], F32)
+            nc.scalar.mul(out=scaled[:], in_=scores[unit, half][:], mul=1.0 / TEMPERATURE)
+            nc.gpsimd.tensor_tensor(
+                out=masked[unit][:, keys],
+                in0=scaled[:],
+                in1=mask_sb[:, unit % Q_TILES, keys],
+                op=ALU.mult,
+            )
+
+        def row_maximum(unit):
+            minus_max = units.tile([P, 1], F32)
+            nc.vector.tensor_reduce(
+                out=minus_max[:],
+                in_=masked[unit][:],
+                axis=mybir.AxisListType.X,
+                op=ALU.max,
+                negate=True,
+            )
+            neg_max[unit] = minus_max
+
+        def exponentials(unit):
+            group, member = divmod(unit, GROUP)
+            if member == 0:
+                e_sums = groups.tile([P, GROUP], F32)
+                row_sums[group] = e_sums
+            e_bf16 = units.tile([P, S], BF16)
+            nc.scalar.activation(
+                out=e_bf16[:],
+                in_=masked[unit][:],
+                func=ACT.Exp,
+                bias=neg_max[unit][:],
+                scale=1.0,
+                accum_out=row_sums[group][:, member : member + 1],
+            )
+            e_rows[unit] = e_bf16
+
+        def transpose_e(unit):
+            e_words = e_rows[unit][:].bitcast(F32)
+            e_words_t = e_t_psum.tile([P, WORD_BLOCKS, P], F32)
+            for c in range(WORD_BLOCKS):
+                g, u = divmod(c, PAIR)
+                first = g * PAIR * P + u
+                nc.tensor.transpose(
+                    e_words_t[:, c, :],
+                    e_words[:, first : (g + 1) * PAIR * P : PAIR],
+                    ident_f32[:],
+                )
+            e_t[unit] = e_words_t
+
+        def regroup_e(unit):
+            group, member = divmod(unit, GROUP)
+            if member == 0:
+                grouped = groups.tile([P, GROUP, PASSES, P, PACK], BF16, align_bytes=64)
+                e_grouped[group] = grouped
+            nc.scalar.copy(
+                out=e_grouped[group][:, member].bitcast(F32),
+                in_=e_t[unit][:].rearrange("p (g u) n -> p g n u", u=PAIR),
+            )
+
+        def multiply_e_v(group):
+            head = group * GROUP // Q_TILES
+            codes = groups.tile([P, GROUP, PASSES, P], U32, align_bytes=64, name="e_code_words")
+            scale_plane = groups.tile(
+                [P, GROUP, PASSES, P], U8, align_bytes=64, name="e_scale_plane"
+            )
+            nc.vector.quantize_mx(
+                out=codes[:].rearrange("p m g n -> p (m g n)").bitcast(FP8X4),
+                scales=scale_plane[:].rearrange("p m g n -> p (m g n)"),
+                in_=e_grouped[group][:].rearrange("p m g n t -> p (m g n t)"),
+            )
+            pv_bank = shared_psum.tile([P, GROUP, D], F32, tag="shared_bank")
+            for member in range(GROUP):
+                for g in range(PASSES):
+                    nc.tensor.matmul_mx(
+                        out=pv_bank[:, member, :],
+                        lhsT=codes[:, member, g, :].bitcast(FP8X4),
+                        lhsT_scale=scale_plane[:, member, g, :],
+                        rhs=v_codes[head][:, g, :].bitcast(FP8X4),
+                        rhs_scale=v_scales[head][:, g, :],
+                        start=(g == 0),
+                        stop=(g == PASSES - 1),
+                    )
+            pv[group] = pv_bank
+            inverse = groups.tile([P, GROUP], F32)
+            nc.vector.reciprocal(out=inverse[:], in_=row_sums[group][:])
+            row_sums[group] = inverse
+
+        def divide_and_store(group):
+            head, first_tile = divmod(group * GROUP, Q_TILES)
+            out_sb = groups.tile([P, GROUP, D], F32)
+            for member in range(GROUP):
+                nc.scalar.activation(
+                    out=out_sb[:, member, :],
+                    in_=pv[group][:, member, :],
+                    func=ACT.Copy,
+                    scale=row_sums[group][:, member : member + 1],
+                )
+            nc.sync.dma_start(
+                out=out_heads[head][:, first_tile : first_tile + GROUP, :], in_=out_sb[:]
+            )
+
+        def is_unit(index):
+            return 0 <= index < UNITS
+
+        def starts_head(index):
+            return is_unit(index) and index % Q_TILES == 0
+
+        def ends_group(index):
+            return is_unit(index) and index % GROUP == GROUP - 1
+
+        ctx.enter_context(tc.manual_schedule())
+        for step in range(-LOAD_LEAD, UNITS + OUT_LAG):
+            if starts_head(step + LOAD_LEAD):
+                load_head((step + LOAD_LEAD) // Q_TILES)
+            if 0 <= step + MASK_LEAD < Q_TILES:
+                tile_index = step + MASK_LEAD
+                nc.sync.dma_start(out=mask_sb[:, tile_index, :], in_=mask_tiles[0, :, tile_index, :])
+
+            if is_unit(step - E_T_LAG):
+                transpose_e(step - E_T_LAG)
+            if is_unit(step + SCORE_LEAD):
+                multiply_q_k(step + SCORE_LEAD)
+
+            if is_unit(step):
+                mask_scores(step, FIRST_HALF)
+            if is_unit(step - MAX_LAG):
+                row_maximum(step - MAX_LAG)
+            if ends_group(step - PV_LAG):
+                multiply_e_v((step - PV_LAG) // GROUP)
+            if starts_head(step + V_QUANT_LEAD):
+                quantise_v((step + V_QUANT_LEAD) // Q_TILES)
+            if starts_head(step + V_GROUP_LEAD):
+                regroup_v((step + V_GROUP_LEAD) // Q_TILES)
+            if is_unit(step) and not takes_detour(step):
+                mask_scores(step, LAST_HALF)
+
+            if is_unit(step - EXP_LAG):
+                exponentials(step - EXP_LAG)
+            if is_unit(step + DETOUR_LEAD) and takes_detour(step + DETOUR_LEAD):
+                mask_scores_on_detour(step + DETOUR_LEAD, LAST_HALF)
+            if is_unit(step - E_T_LAG):
+                regroup_e(step - E_T_LAG)
+            if ends_group(step - OUT_LAG):
+                divide_and_store((step - OUT_LAG) // GROUP)
+            if starts_head(step + Q_T_LEAD):
+                transpose_q((step + Q_T_LEAD) // Q_TILES)
+            if starts_head(step + K_T_LEAD):
+                transpose_k((step + K_T_LEAD) // Q_TILES)

@@ -16,12 +16,11 @@ HEADS = 16
 S = 1024
 D = 128
 TEMPERATURE = 8.0
-Q_TILES = S // P
-UNITS = HEADS * Q_TILES
+TILES = S // P
+UNITS = HEADS * TILES
 GROUP = 4
 BANK = 512
 HALVES = S // BANK
-FIRST_HALF, LAST_HALF = 0, HALVES - 1
 PACK = 4
 K_PASS = P * PACK
 PASSES = S // K_PASS
@@ -30,83 +29,114 @@ WORD_BLOCKS = S // (PAIR * P)
 
 FLOPS = 2 * 2 * HEADS * S * S * D
 
-DETOURS = 2
-
-LOAD_LEAD = 16
-MASK_LEAD = 15
-Q_T_LEAD = 8
-K_T_LEAD = 4
-V_GROUP_LEAD = 10
-V_QUANT_LEAD = 2
-SCORE_LEAD = 2
-DETOUR_LEAD = 1
-MAX_LAG = 1
-EXP_LAG = 2
-E_T_LAG = 3
-PV_LAG = 7
-OUT_LAG = 8
+TENSOR_TILES = (0, 2, 3, 5, 6)
+BIG = 2.0**120
+FIRST_TENSOR_HEAD = 1
+DETOUR_TILES = (1, 4, 7)
+TICKS = 4
+VECTOR_BANKS = 2
+TENSOR_BANKS = 4
+E_BANKS = 2
+PV_WITH_E = True
 
 
 def tile_scaleddotproductattention_pa_kernel(tc, q, k, v, mask, out):
     nc = tc.nc
 
-    q_heads = q.rearrange("b h (p t) d -> (b h) p t d", t=Q_TILES)
+    q_heads = q.rearrange("b h (p t) d -> (b h) p t d", t=TILES)
     k_heads = k.rearrange("b h (t p) d -> (b h) p t d", p=P)
-    mask_tiles = mask.rearrange("a b (p t) k -> (a b) p t k", t=Q_TILES)
-    out_heads = out.rearrange("b h (p t) d -> (b h) p t d", t=Q_TILES)
-    v_heads = v.rearrange("b h (g p t) d -> (b h) p g t d", p=P, t=PACK)
+    mask_tiles = mask.rearrange("a b (p t) k -> (a b) p t k", t=TILES)
+    out_heads = out.rearrange("b h (p t) d -> (b h) p t d", t=TILES)
+    v_heads = v.rearrange("b h (g p n) d -> (b h) p g n d", p=P, n=PACK)
 
     with ExitStack() as ctx:
         consts = ctx.enter_context(tc.tile_pool(name="consts", bufs=1))
         heads = ctx.enter_context(tc.tile_pool(name="heads", bufs=3))
         groups = ctx.enter_context(tc.tile_pool(name="groups", bufs=3))
-        units = ctx.enter_context(tc.tile_pool(name="units", bufs=3))
-        masked_pool = ctx.enter_context(tc.tile_pool(name="masked_pool", bufs=5))
-        score_psum = ctx.enter_context(tc.psum_pool(name="score_psum", bufs=3 * HALVES))
-        e_t_psum = ctx.enter_context(tc.psum_pool(name="e_t_psum", bufs=1))
-        shared_psum = ctx.enter_context(tc.psum_pool(name="shared_psum", bufs=1))
+        units = ctx.enter_context(tc.tile_pool(name="units", bufs=4))
+        stats = ctx.enter_context(tc.tile_pool(name="stats", bufs=8))
+        vector_psum = ctx.enter_context(tc.psum_pool(name="vector_psum", bufs=VECTOR_BANKS))
+        tensor_psum = ctx.enter_context(tc.psum_pool(name="tensor_psum", bufs=TENSOR_BANKS))
+        e_psum = ctx.enter_context(tc.psum_pool(name="e_psum", bufs=E_BANKS))
+        pv_psum = e_psum if PV_WITH_E else vector_psum
+        pv_tag = "e_bank" if PV_WITH_E else "vector_bank"
 
         ident_bf16 = consts.tile([P, P], BF16)
         make_identity(nc, ident_bf16[:])
         ident_f32 = consts.tile([P, P], F32)
         make_identity(nc, ident_f32[:])
-        mask_sb = consts.tile([P, Q_TILES, S], BF16)
+        mask_sb = consts.tile([P, TILES, S], BF16)
+        plus_big = consts.tile([P, len(TENSOR_TILES), TILES, P], F32)
+        minus_big = consts.tile([P, len(TENSOR_TILES), TILES, P], F32)
 
         q_rows, k_rows, v_rows, v_grouped = {}, {}, {}, {}
-        q_t, k_t, v_codes, v_scales = {}, {}, {}, {}
-        e_grouped, row_sums, pv = {}, {}, {}
+        q_banks, k_banks, q_t, k_t, v_codes, v_scales = {}, {}, {}, {}, {}, {}
+        e_grouped, e_codes, e_scales, row_sums, pv = {}, {}, {}, {}, {}
         scores, masked, neg_max, e_rows, e_t = {}, {}, {}, {}, {}
+        first_max = {}
+        sums = {}
 
         def load_head(head):
-            q_in = heads.tile([P, Q_TILES, D], BF16)
+            q_in = heads.tile([P, TILES, D], BF16)
             nc.sync.dma_start(out=q_in[:], in_=q_heads[head])
-            k_in = heads.tile([P, Q_TILES, D], BF16)
+            k_in = heads.tile([P, TILES, D], BF16)
             nc.sync.dma_start(out=k_in[:], in_=k_heads[head])
+            q_rows[head], k_rows[head] = q_in, k_in
+
+        def load_v(head):
             v_in = heads.tile([P, PASSES, PACK, D], BF16)
             nc.sync.dma_start(out=v_in[:], in_=v_heads[head])
-            q_rows[head], k_rows[head], v_rows[head] = q_in, k_in, v_in
+            v_rows[head] = v_in
 
-        def transpose_rows(rows):
-            t_bank = shared_psum.tile([P, Q_TILES, P], BF16, tag="shared_bank")
-            for tile_index in range(Q_TILES):
-                nc.tensor.transpose(t_bank[:, tile_index, :], rows[:, tile_index, :], ident_bf16[:])
+        def load_mask(tile):
+            nc.sync.dma_start(out=mask_sb[:, tile, :], in_=mask_tiles[0, :, tile, :])
+
+        def transpose_blocks(rows):
+            t_bank = vector_psum.tile([P, TILES, P], BF16, tag="vector_bank")
+            for block in range(TILES):
+                nc.tensor.transpose(t_bank[:, block, :], rows[:, block, :], ident_bf16[:])
             return t_bank
 
-        def transpose_q(head):
-            q_cols = heads.tile([P, Q_TILES, P], BF16)
-            nc.scalar.copy(out=q_cols[:], in_=transpose_rows(q_rows[head])[:])
+        def transpose_q_k(head):
+            q_banks[head] = transpose_blocks(q_rows[head])
+            k_banks[head] = transpose_blocks(k_rows[head])
+
+        def take_q(head):
+            q_cols = heads.tile([P, TILES, P], BF16)
+            nc.vector.tensor_scalar(
+                out=q_cols[:],
+                in0=q_banks[head][:],
+                scalar1=1.0 / TEMPERATURE,
+                scalar2=None,
+                op0=ALU.mult,
+            )
             q_t[head] = q_cols
 
-        def transpose_k(head):
-            k_cols = heads.tile([P, Q_TILES, P], BF16)
-            nc.scalar.copy(out=k_cols[:], in_=transpose_rows(k_rows[head])[:])
+        def take_k(head):
+            k_cols = heads.tile([P, TILES, P], BF16)
+            nc.scalar.copy(out=k_cols[:], in_=k_banks[head][:])
             k_t[head] = k_cols
+
+        def make_tables(index):
+            mask_rows = mask_sb[:, TENSOR_TILES[index], :].rearrange("p (t k) -> p t k", k=P)
+            t_bank = transpose_blocks(mask_rows)
+            mask_t = heads.tile([P, TILES, P], BF16)
+            nc.scalar.copy(out=mask_t[:], in_=t_bank[:])
+            for table, big in ((plus_big, BIG), (minus_big, -BIG)):
+                nc.gpsimd.tensor_scalar(
+                    out=table[:, index],
+                    in0=mask_t[:],
+                    scalar1=-big,
+                    scalar2=big,
+                    op0=ALU.mult,
+                    op1=ALU.add,
+                )
 
         def regroup_v(head):
             grouped = consts.tile([P, PASSES, D, PACK], BF16, align_bytes=64, name="v_grouped_keys")
             nc.gpsimd.tensor_scalar(
                 out=grouped[:],
-                in0=v_rows[head][:].rearrange("p g t d -> p g d t"),
+                in0=v_rows[head][:].rearrange("p g n d -> p g d n"),
                 scalar1=1.0,
                 scalar2=0.0,
                 op0=ALU.mult,
@@ -120,53 +150,75 @@ def tile_scaleddotproductattention_pa_kernel(tc, q, k, v, mask, out):
             nc.vector.quantize_mx(
                 out=codes[:].rearrange("p g d -> p (g d)").bitcast(FP8X4),
                 scales=scale_plane[:].rearrange("p g d -> p (g d)"),
-                in_=v_grouped[head][:].rearrange("p g d t -> p (g d t)"),
+                in_=v_grouped[head][:].rearrange("p g d n -> p (g d n)"),
             )
             v_codes[head], v_scales[head] = codes, scale_plane
 
+        def by_tensor(unit):
+            head, tile = divmod(unit, TILES)
+            return head >= FIRST_TENSOR_HEAD and tile in TENSOR_TILES
+
         def takes_detour(unit):
-            return unit % GROUP < DETOURS
+            return not by_tensor(unit) and unit % TILES in DETOUR_TILES
 
-        def multiply_q_k(unit):
-            head, tile_index = divmod(unit, Q_TILES)
-            masked_rows = masked_pool.tile([P, S], F32)
-            masked[unit] = masked_rows
-            for half in range(HALVES):
-                score_bank = score_psum.tile([P, BANK], F32)
-                key_tiles = slice(half * BANK // P, (half + 1) * BANK // P)
-                nc.tensor.matmul(
-                    out=score_bank[:],
-                    lhsT=q_t[head][:, tile_index, :],
-                    rhs=k_t[head][:, key_tiles, :].rearrange("d t p -> d (t p)"),
-                    start=True,
-                    stop=True,
-                )
-                scores[unit, half] = score_bank
-
-        def mask_scores(unit, half):
-            keys = slice(half * BANK, (half + 1) * BANK)
-            nc.vector.scalar_tensor_tensor(
-                out=masked[unit][:, keys],
-                in0=scores[unit, half][:],
-                scalar=1.0 / TEMPERATURE,
-                in1=mask_sb[:, unit % Q_TILES, keys],
-                op0=ALU.mult,
-                op1=ALU.mult,
+        def multiply_q_k(unit, half, bank, stop):
+            head, tile = divmod(unit, TILES)
+            key_tiles = slice(half * BANK // P, (half + 1) * BANK // P)
+            nc.tensor.matmul(
+                out=bank,
+                lhsT=q_t[head][:, tile, :],
+                rhs=k_t[head][:, key_tiles, :].rearrange("d t p -> d (t p)"),
+                start=True,
+                stop=stop,
             )
 
-        def mask_scores_on_detour(unit, half):
+        def scores_for_vector(unit):
+            for half in range(HALVES):
+                score_bank = vector_psum.tile([P, BANK], F32, tag="vector_bank")
+                multiply_q_k(unit, half, score_bank[:], True)
+                scores[unit, half] = score_bank
+            masked_rows = units.tile([P, S], F32)
+            masked[unit] = masked_rows
+
+        def scores_masked_by_tensor(unit, half):
+            index = TENSOR_TILES.index(unit % TILES)
+            if True:
+                score_bank = tensor_psum.tile([P, BANK // P, P], F32)
+                multiply_q_k(unit, half, score_bank[:].rearrange("p t k -> p (t k)"), False)
+                for table in (plus_big, minus_big):
+                    for t in range(BANK // P):
+                        nc.tensor.matmul(
+                            out=score_bank[:, t, :],
+                            lhsT=table[:, index, half * BANK // P + t, :],
+                            rhs=ident_f32[:],
+                            start=False,
+                            stop=(table is minus_big and t == BANK // P - 1),
+                            is_transpose=True,
+                        )
+                scores[unit, half] = score_bank
+
+        def mask_by_vector(unit, half):
             keys = slice(half * BANK, (half + 1) * BANK)
-            scaled = units.tile([P, BANK], F32)
-            nc.scalar.mul(out=scaled[:], in_=scores[unit, half][:], mul=1.0 / TEMPERATURE)
+            nc.vector.tensor_tensor(
+                out=masked[unit][:, keys],
+                in0=scores[unit, half][:],
+                in1=mask_sb[:, unit % TILES, keys],
+                op=ALU.mult,
+            )
+
+        def mask_on_detour(unit):
+            keys = slice((HALVES - 1) * BANK, S)
+            unmasked = units.tile([P, BANK], F32)
+            nc.scalar.copy(out=unmasked[:], in_=scores[unit, HALVES - 1][:])
             nc.gpsimd.tensor_tensor(
                 out=masked[unit][:, keys],
-                in0=scaled[:],
-                in1=mask_sb[:, unit % Q_TILES, keys],
+                in0=unmasked[:],
+                in1=mask_sb[:, unit % TILES, keys],
                 op=ALU.mult,
             )
 
         def row_maximum(unit):
-            minus_max = units.tile([P, 1], F32)
+            minus_max = stats.tile([P, 1], F32)
             nc.vector.tensor_reduce(
                 out=minus_max[:],
                 in_=masked[unit][:],
@@ -176,33 +228,65 @@ def tile_scaleddotproductattention_pa_kernel(tc, q, k, v, mask, out):
             )
             neg_max[unit] = minus_max
 
+        def first_half_maximum(unit):
+            half_max = stats.tile([P, 1], F32)
+            nc.vector.tensor_reduce(
+                out=half_max[:],
+                in_=scores[unit, 0][:],
+                axis=mybir.AxisListType.XY,
+                op=ALU.max,
+                negate=True,
+            )
+            first_max[unit] = half_max
+
+        def last_half_maximum(unit):
+            minus_max = stats.tile([P, 1], F32)
+            negated = units.tile([P, BANK], BF16)
+            nc.vector.tensor_scalar(
+                out=negated[:],
+                in0=scores[unit, HALVES - 1][:].rearrange("p t k -> p (t k)"),
+                scalar1=-1.0,
+                scalar2=first_max[unit][:],
+                op0=ALU.mult,
+                op1=ALU.min,
+                accum_out=minus_max[:],
+            )
+            neg_max[unit] = minus_max
+
         def exponentials(unit):
             group, member = divmod(unit, GROUP)
-            if member == 0:
-                e_sums = groups.tile([P, GROUP], F32)
+            if group not in row_sums:
+                e_sums = stats.tile([P, GROUP, HALVES], F32)
+                nc.gpsimd.memset(e_sums[:], 0.0)
                 row_sums[group] = e_sums
             e_bf16 = units.tile([P, S], BF16)
-            nc.scalar.activation(
-                out=e_bf16[:],
-                in_=masked[unit][:],
-                func=ACT.Exp,
-                bias=neg_max[unit][:],
-                scale=1.0,
-                accum_out=row_sums[group][:, member : member + 1],
-            )
+            if by_tensor(unit):
+                pieces = [scores[unit, half][:].rearrange("p t k -> p (t k)") for half in range(HALVES)]
+            else:
+                pieces = [masked[unit][:]]
+            width = S // len(pieces)
+            for half, score_keys in enumerate(pieces):
+                nc.scalar.activation(
+                    out=e_bf16[:, half * width : (half + 1) * width].rearrange(
+                        "p (u x j) -> p u x j", u=PAIR, j=PAIR
+                    ),
+                    in_=score_keys.rearrange("p (x u j) -> p u x j", u=PAIR, j=PAIR),
+                    func=ACT.Exp,
+                    bias=neg_max[unit][:],
+                    scale=1.0,
+                    accum_out=row_sums[group][:, member, half : half + 1],
+                )
             e_rows[unit] = e_bf16
 
         def transpose_e(unit):
             e_words = e_rows[unit][:].bitcast(F32)
-            e_words_t = e_t_psum.tile([P, WORD_BLOCKS, P], F32)
-            for c in range(WORD_BLOCKS):
-                g, u = divmod(c, PAIR)
-                first = g * PAIR * P + u
-                nc.tensor.transpose(
-                    e_words_t[:, c, :],
-                    e_words[:, first : (g + 1) * PAIR * P : PAIR],
-                    ident_f32[:],
-                )
+            e_words_t = e_psum.tile([P, PASSES, PAIR, P], F32, tag="e_bank")
+            for u in range(PAIR):
+                for g in range(PASSES):
+                    first = (g * PAIR + u if by_tensor(unit) else u * PASSES + g) * P
+                    nc.tensor.transpose(
+                        e_words_t[:, g, u, :], e_words[:, first : first + P], ident_f32[:]
+                    )
             e_t[unit] = e_words_t
 
         def regroup_e(unit):
@@ -212,11 +296,10 @@ def tile_scaleddotproductattention_pa_kernel(tc, q, k, v, mask, out):
                 e_grouped[group] = grouped
             nc.scalar.copy(
                 out=e_grouped[group][:, member].bitcast(F32),
-                in_=e_t[unit][:].rearrange("p (g u) n -> p g n u", u=PAIR),
+                in_=e_t[unit][:].rearrange("p g u n -> p g n u"),
             )
 
-        def multiply_e_v(group):
-            head = group * GROUP // Q_TILES
+        def quantise_e(group):
             codes = groups.tile([P, GROUP, PASSES, P], U32, align_bytes=64, name="e_code_words")
             scale_plane = groups.tile(
                 [P, GROUP, PASSES, P], U8, align_bytes=64, name="e_scale_plane"
@@ -226,7 +309,12 @@ def tile_scaleddotproductattention_pa_kernel(tc, q, k, v, mask, out):
                 scales=scale_plane[:].rearrange("p m g n -> p (m g n)"),
                 in_=e_grouped[group][:].rearrange("p m g n t -> p (m g n t)"),
             )
-            pv_bank = shared_psum.tile([P, GROUP, D], F32, tag="shared_bank")
+            e_codes[group], e_scales[group] = codes, scale_plane
+
+        def multiply_e_v(group):
+            head = group * GROUP // TILES
+            codes, scale_plane = e_codes[group], e_scales[group]
+            pv_bank = pv_psum.tile([P, GROUP, D], F32, tag=pv_tag)
             for member in range(GROUP):
                 for g in range(PASSES):
                     nc.tensor.matmul_mx(
@@ -239,20 +327,28 @@ def tile_scaleddotproductattention_pa_kernel(tc, q, k, v, mask, out):
                         stop=(g == PASSES - 1),
                     )
             pv[group] = pv_bank
-            inverse = groups.tile([P, GROUP], F32)
-            nc.vector.reciprocal(out=inverse[:], in_=row_sums[group][:])
+
+        def add_row_sums(group):
+            row_totals = stats.tile([P, GROUP], F32)
+            nc.vector.tensor_reduce(
+                out=row_totals[:], in_=row_sums[group][:], axis=mybir.AxisListType.X, op=ALU.add
+            )
+            sums[group] = row_totals
+
+        def invert(group):
+            inverse = stats.tile([P, GROUP], F32)
+            nc.vector.reciprocal(out=inverse[:], in_=sums[group][:])
             row_sums[group] = inverse
 
         def divide_and_store(group):
-            head, first_tile = divmod(group * GROUP, Q_TILES)
+            head, first_tile = divmod(group * GROUP, TILES)
             out_sb = groups.tile([P, GROUP, D], F32)
-            for member in range(GROUP):
-                nc.scalar.activation(
-                    out=out_sb[:, member, :],
-                    in_=pv[group][:, member, :],
-                    func=ACT.Copy,
-                    scale=row_sums[group][:, member : member + 1],
-                )
+            nc.vector.tensor_tensor(
+                out=out_sb[:],
+                in0=pv[group][:],
+                in1=row_sums[group][:].unsqueeze(2).to_broadcast([P, GROUP, D]),
+                op=ALU.mult,
+            )
             nc.sync.dma_start(
                 out=out_heads[head][:, first_tile : first_tile + GROUP, :], in_=out_sb[:]
             )
@@ -260,47 +356,84 @@ def tile_scaleddotproductattention_pa_kernel(tc, q, k, v, mask, out):
         def is_unit(index):
             return 0 <= index < UNITS
 
-        def starts_head(index):
-            return is_unit(index) and index % Q_TILES == 0
-
         def ends_group(index):
             return is_unit(index) and index % GROUP == GROUP - 1
 
         ctx.enter_context(tc.manual_schedule())
-        for step in range(-LOAD_LEAD, UNITS + OUT_LAG):
-            if starts_head(step + LOAD_LEAD):
-                load_head((step + LOAD_LEAD) // Q_TILES)
-            if 0 <= step + MASK_LEAD < Q_TILES:
-                tile_index = step + MASK_LEAD
-                nc.sync.dma_start(out=mask_sb[:, tile_index, :], in_=mask_tiles[0, :, tile_index, :])
+        load_head(0)
+        load_mask(0)
+        load_mask(1)
+        load_v(0)
+        for tile in range(2, TILES):
+            load_mask(tile)
+        load_head(1)
+        load_v(1)
+        transpose_q_k(0)
+        take_q(0)
+        take_k(0)
+        regroup_v(0)
 
-            if is_unit(step - E_T_LAG):
-                transpose_e(step - E_T_LAG)
-            if is_unit(step + SCORE_LEAD):
-                multiply_q_k(step + SCORE_LEAD)
+        def of_tensor(stage, *args):
+            return lambda unit: stage(unit, *args) if by_tensor(unit) else None
 
-            if is_unit(step):
-                mask_scores(step, FIRST_HALF)
-            if is_unit(step - MAX_LAG):
-                row_maximum(step - MAX_LAG)
-            if ends_group(step - PV_LAG):
-                multiply_e_v((step - PV_LAG) // GROUP)
-            if starts_head(step + V_QUANT_LEAD):
-                quantise_v((step + V_QUANT_LEAD) // Q_TILES)
-            if starts_head(step + V_GROUP_LEAD):
-                regroup_v((step + V_GROUP_LEAD) // Q_TILES)
-            if is_unit(step) and not takes_detour(step):
-                mask_scores(step, LAST_HALF)
+        def of_first_head(stage):
+            return lambda unit: stage(unit) if unit < TILES else None
 
-            if is_unit(step - EXP_LAG):
-                exponentials(step - EXP_LAG)
-            if is_unit(step + DETOUR_LEAD) and takes_detour(step + DETOUR_LEAD):
-                mask_scores_on_detour(step + DETOUR_LEAD, LAST_HALF)
-            if is_unit(step - E_T_LAG):
-                regroup_e(step - E_T_LAG)
-            if ends_group(step - OUT_LAG):
-                divide_and_store((step - OUT_LAG) // GROUP)
-            if starts_head(step + Q_T_LEAD):
-                transpose_q((step + Q_T_LEAD) // Q_TILES)
-            if starts_head(step + K_T_LEAD):
-                transpose_k((step + K_T_LEAD) // Q_TILES)
+        def of_later_heads(stage):
+            return lambda unit: stage(unit) if unit >= TILES and not by_tensor(unit) else None
+
+        def of_vector(stage, *args):
+            return lambda unit: None if by_tensor(unit) else stage(unit, *args)
+
+        def mask_last_half(unit):
+            if takes_detour(unit):
+                return
+            mask_by_vector(unit, HALVES - 1)
+
+        def of_detour(stage):
+            return lambda unit: stage(unit) if takes_detour(unit) else None
+
+        def of_group(stage):
+            return lambda unit: stage(unit // GROUP) if unit % GROUP == GROUP - 1 else None
+
+        def of_head(stage, tile, first=0):
+            return lambda unit: stage(unit // TILES + first) if unit % TILES == tile and unit // TILES + first < HEADS else None
+
+        def tables(unit):
+            if unit < len(TENSOR_TILES):
+                make_tables(unit)
+
+        stages = [
+            (1, of_head(take_q, 3, 1)),
+            (1, of_head(take_k, 3, 1)),
+            (-7, of_first_head(scores_for_vector)),
+            (-12, of_later_heads(scores_for_vector)),
+            (-7, of_vector(mask_by_vector, 0)),
+            (-6, of_vector(mask_last_half)),
+            (-5, of_detour(mask_on_detour)),
+            (-5, of_tensor(scores_masked_by_tensor, 0)),
+            (-4, of_tensor(scores_masked_by_tensor, 1)),
+            (0, of_tensor(first_half_maximum)),
+            (1, of_tensor(last_half_maximum)),
+            (2, of_vector(row_maximum)),
+            (4, of_tensor(exponentials)),
+            (5, of_vector(exponentials)),
+            (8, transpose_e),
+            (11, regroup_e),
+            (10, of_group(add_row_sums)),
+            (13, of_group(quantise_e)),
+            (14, of_group(invert)),
+            (17, of_group(multiply_e_v)),
+            (19, of_group(divide_and_store)),
+            (0, of_head(load_head, 0, 2)),
+            (0, of_head(load_v, 0, 2)),
+            (0, of_head(transpose_q_k, 3, 1)),
+            (0, of_head(regroup_v, 7, 1)),
+            (0, of_head(quantise_v, 2)),
+            (0, tables),
+        ]
+        for tick in range(-TICKS * 4, TICKS * (UNITS + 8)):
+            for offset, stage in stages:
+                unit, rest = divmod(tick - offset, TICKS)
+                if rest == 0 and is_unit(unit):
+                    stage(unit)

@@ -29,10 +29,10 @@ WORD_BLOCKS = S // (PAIR * P)
 
 FLOPS = 2 * 2 * HEADS * S * S * D
 
-TENSOR_TILES = (0, 2, 3, 5, 6)
+TENSOR_TILES = (1, 3, 5, 7)
 BIG = 2.0**120
 FIRST_TENSOR_HEAD = 1
-DETOUR_TILES = (1, 4, 7)
+DETOUR_TILES = (0, 2, 4, 6)
 TICKS = 4
 VECTOR_BANKS = 2
 TENSOR_BANKS = 4
@@ -159,7 +159,7 @@ def tile_scaleddotproductattention_pa_kernel(tc, q, k, v, mask, out):
             return head >= FIRST_TENSOR_HEAD and tile in TENSOR_TILES
 
         def takes_detour(unit):
-            return not by_tensor(unit) and unit % TILES in DETOUR_TILES
+            return unit % TILES in DETOUR_TILES
 
         def multiply_q_k(unit, half, bank, stop):
             head, tile = divmod(unit, TILES)
@@ -180,22 +180,28 @@ def tile_scaleddotproductattention_pa_kernel(tc, q, k, v, mask, out):
             masked_rows = units.tile([P, S], F32)
             masked[unit] = masked_rows
 
-        def scores_masked_by_tensor(unit, half):
+        def scores_for_tensor(unit):
+            for half in range(HALVES):
+                score_bank = tensor_psum.tile([P, BANK], F32, tag="tensor_bank")
+                multiply_q_k(unit, half, score_bank[:], not by_tensor(unit))
+                scores[unit, half] = score_bank
+            if not by_tensor(unit):
+                masked_rows = units.tile([P, S], F32)
+                masked[unit] = masked_rows
+
+        def mask_by_tensor(unit):
             index = TENSOR_TILES.index(unit % TILES)
-            if True:
-                score_bank = tensor_psum.tile([P, BANK // P, P], F32)
-                multiply_q_k(unit, half, score_bank[:].rearrange("p t k -> p (t k)"), False)
+            for half in range(HALVES):
                 for table in (plus_big, minus_big):
                     for t in range(BANK // P):
                         nc.tensor.matmul(
-                            out=score_bank[:, t, :],
+                            out=scores[unit, half][:, t * P : (t + 1) * P],
                             lhsT=table[:, index, half * BANK // P + t, :],
                             rhs=ident_f32[:],
                             start=False,
                             stop=(table is minus_big and t == BANK // P - 1),
                             is_transpose=True,
                         )
-                scores[unit, half] = score_bank
 
         def mask_by_vector(unit, half):
             keys = slice(half * BANK, (half + 1) * BANK)
@@ -233,7 +239,7 @@ def tile_scaleddotproductattention_pa_kernel(tc, q, k, v, mask, out):
             nc.vector.tensor_reduce(
                 out=half_max[:],
                 in_=scores[unit, 0][:],
-                axis=mybir.AxisListType.XY,
+                axis=mybir.AxisListType.X,
                 op=ALU.max,
                 negate=True,
             )
@@ -244,7 +250,7 @@ def tile_scaleddotproductattention_pa_kernel(tc, q, k, v, mask, out):
             negated = units.tile([P, BANK], BF16)
             nc.vector.tensor_scalar(
                 out=negated[:],
-                in0=scores[unit, HALVES - 1][:].rearrange("p t k -> p (t k)"),
+                in0=scores[unit, HALVES - 1][:],
                 scalar1=-1.0,
                 scalar2=first_max[unit][:],
                 op0=ALU.mult,
@@ -253,15 +259,16 @@ def tile_scaleddotproductattention_pa_kernel(tc, q, k, v, mask, out):
             )
             neg_max[unit] = minus_max
 
+        def open_row_sums(group):
+            e_sums = stats.tile([P, GROUP, HALVES], F32)
+            nc.gpsimd.memset(e_sums[:], 0.0)
+            row_sums[group] = e_sums
+
         def exponentials(unit):
             group, member = divmod(unit, GROUP)
-            if group not in row_sums:
-                e_sums = stats.tile([P, GROUP, HALVES], F32)
-                nc.gpsimd.memset(e_sums[:], 0.0)
-                row_sums[group] = e_sums
             e_bf16 = units.tile([P, S], BF16)
             if by_tensor(unit):
-                pieces = [scores[unit, half][:].rearrange("p t k -> p (t k)") for half in range(HALVES)]
+                pieces = [scores[unit, half][:] for half in range(HALVES)]
             else:
                 pieces = [masked[unit][:]]
             width = S // len(pieces)
@@ -353,11 +360,9 @@ def tile_scaleddotproductattention_pa_kernel(tc, q, k, v, mask, out):
                 out=out_heads[head][:, first_tile : first_tile + GROUP, :], in_=out_sb[:]
             )
 
-        def is_unit(index):
-            return 0 <= index < UNITS
-
-        def ends_group(index):
-            return is_unit(index) and index % GROUP == GROUP - 1
+        def ends_head_at(pair, offset):
+            head, rest = divmod(pair - offset, TILES // 2)
+            return head if rest == 0 and 0 <= head < HEADS else None
 
         ctx.enter_context(tc.manual_schedule())
         load_head(0)
@@ -373,67 +378,67 @@ def tile_scaleddotproductattention_pa_kernel(tc, q, k, v, mask, out):
         take_k(0)
         regroup_v(0)
 
-        def of_tensor(stage, *args):
-            return lambda unit: stage(unit, *args) if by_tensor(unit) else None
+        PAIRS = UNITS // 2
 
-        def of_first_head(stage):
-            return lambda unit: stage(unit) if unit < TILES else None
+        def run(pairs, unit_of_pair, stage, *args):
+            if 0 <= pairs < PAIRS:
+                stage(2 * pairs + unit_of_pair, *args)
 
-        def of_later_heads(stage):
-            return lambda unit: stage(unit) if unit >= TILES and not by_tensor(unit) else None
+        for j in range(-2, PAIRS + 4):
+            head, place = divmod(j, TILES // 2)
+            group = (j - 1) // 2
+            nxt = head + 1
+            prepares = place == 2 and 1 <= nxt < HEADS
 
-        def of_vector(stage, *args):
-            return lambda unit: None if by_tensor(unit) else stage(unit, *args)
+            run(j - 1, 1, transpose_e)
+            if prepares:
+                transpose_q_k(nxt)
 
-        def mask_last_half(unit):
-            if takes_detour(unit):
-                return
-            mask_by_vector(unit, HALVES - 1)
+            if j % 2 == 0 and 0 <= (j - 3) // 2 < UNITS // GROUP and j >= 3:
+                divide_and_store((j - 3) // 2)
+            if place == 1 and 0 <= head < HEADS:
+                quantise_v(head)
+            if 0 <= j < PAIRS and by_tensor(2 * j + 1):
+                first_half_maximum(2 * j + 1)
+            run(j, 0, row_maximum)
+            if prepares:
+                take_q(nxt)
+            if 0 <= j < PAIRS:
+                if by_tensor(2 * j + 1):
+                    last_half_maximum(2 * j + 1)
+                else:
+                    row_maximum(2 * j + 1)
 
-        def of_detour(stage):
-            return lambda unit: stage(unit) if takes_detour(unit) else None
+            run(j + 1, 0, mask_on_detour)
+            run(j - 1, 0, regroup_e)
+            run(j - 1, 1, regroup_e)
+            if prepares:
+                take_k(nxt)
+            run(j, 0, exponentials)
+            run(j, 1, exponentials)
+            if 0 <= j + 2 < PAIRS and j % 2 == 0:
+                open_row_sums((j + 2) // 2)
+            if place == 3 and 0 <= head < HEADS - 1:
+                regroup_v(head + 1)
+            if 0 <= j < len(TENSOR_TILES):
+                make_tables(j)
+            if place == 0 and 0 <= head < HEADS - 2:
+                load_head(head + 2)
+                load_v(head + 2)
 
-        def of_group(stage):
-            return lambda unit: stage(unit // GROUP) if unit % GROUP == GROUP - 1 else None
+            run(j + 1, 1, scores_for_tensor)
+            if j % 2 == 1 and 0 <= (j - 2) // 2 < UNITS // GROUP:
+                multiply_e_v((j - 2) // 2)
+            run(j + 2, 0, scores_for_vector)
+            if 0 <= j + 1 < PAIRS and by_tensor(2 * j + 3):
+                mask_by_tensor(2 * j + 3)
+            run(j, 0, transpose_e)
 
-        def of_head(stage, tile, first=0):
-            return lambda unit: stage(unit // TILES + first) if unit % TILES == tile and unit // TILES + first < HEADS else None
-
-        def tables(unit):
-            if unit < len(TENSOR_TILES):
-                make_tables(unit)
-
-        stages = [
-            (1, of_head(take_q, 3, 1)),
-            (1, of_head(take_k, 3, 1)),
-            (-7, of_first_head(scores_for_vector)),
-            (-12, of_later_heads(scores_for_vector)),
-            (-7, of_vector(mask_by_vector, 0)),
-            (-6, of_vector(mask_last_half)),
-            (-5, of_detour(mask_on_detour)),
-            (-5, of_tensor(scores_masked_by_tensor, 0)),
-            (-4, of_tensor(scores_masked_by_tensor, 1)),
-            (0, of_tensor(first_half_maximum)),
-            (1, of_tensor(last_half_maximum)),
-            (2, of_vector(row_maximum)),
-            (4, of_tensor(exponentials)),
-            (5, of_vector(exponentials)),
-            (8, transpose_e),
-            (11, regroup_e),
-            (10, of_group(add_row_sums)),
-            (13, of_group(quantise_e)),
-            (14, of_group(invert)),
-            (17, of_group(multiply_e_v)),
-            (19, of_group(divide_and_store)),
-            (0, of_head(load_head, 0, 2)),
-            (0, of_head(load_v, 0, 2)),
-            (0, of_head(transpose_q_k, 3, 1)),
-            (0, of_head(regroup_v, 7, 1)),
-            (0, of_head(quantise_v, 2)),
-            (0, tables),
-        ]
-        for tick in range(-TICKS * 4, TICKS * (UNITS + 8)):
-            for offset, stage in stages:
-                unit, rest = divmod(tick - offset, TICKS)
-                if rest == 0 and is_unit(unit):
-                    stage(unit)
+            if 0 <= j + 1 < PAIRS and not by_tensor(2 * j + 3):
+                mask_by_vector(2 * j + 3, 0)
+                mask_by_vector(2 * j + 3, 1)
+            run(j + 2, 0, mask_by_vector, 0)
+            if j % 2 == 0 and 0 <= (j - 1) // 2 < UNITS // GROUP and j >= 1:
+                add_row_sums((j - 1) // 2)
+                quantise_e((j - 1) // 2)
+                invert((j - 1) // 2)

@@ -73,7 +73,7 @@ def tile_scaleddotproductattention_pa_kernel(tc, q, k, v, mask, out):
         q_banks, k_banks, q_t, k_t, v_codes, v_scales = {}, {}, {}, {}, {}, {}
         e_grouped, e_codes, e_scales, row_sums, pv = {}, {}, {}, {}, {}
         scores, masked, neg_max, e_rows, e_t = {}, {}, {}, {}, {}
-        first_max = {}
+        half_maxima = {}
         sums = {}
 
         def load_head(head):
@@ -234,28 +234,25 @@ def tile_scaleddotproductattention_pa_kernel(tc, q, k, v, mask, out):
             )
             neg_max[unit] = minus_max
 
-        def first_half_maximum(unit):
-            half_max = stats.tile([P, 1], F32)
+        def half_maximum(unit, half):
+            if half == 0:
+                maxima = stats.tile([P, HALVES], F32)
+                half_maxima[unit] = maxima
             nc.vector.tensor_reduce(
-                out=half_max[:],
-                in_=scores[unit, 0][:],
+                out=half_maxima[unit][:, half : half + 1],
+                in_=scores[unit, half][:],
                 axis=mybir.AxisListType.X,
                 op=ALU.max,
                 negate=True,
             )
-            first_max[unit] = half_max
 
-        def last_half_maximum(unit):
+        def combine_half_maxima(unit):
             minus_max = stats.tile([P, 1], F32)
-            negated = units.tile([P, BANK], BF16)
-            nc.vector.tensor_scalar(
-                out=negated[:],
-                in0=scores[unit, HALVES - 1][:],
-                scalar1=-1.0,
-                scalar2=first_max[unit][:],
-                op0=ALU.mult,
-                op1=ALU.min,
-                accum_out=minus_max[:],
+            nc.vector.tensor_reduce(
+                out=minus_max[:],
+                in_=half_maxima[unit][:],
+                axis=mybir.AxisListType.X,
+                op=ALU.min,
             )
             neg_max[unit] = minus_max
 
@@ -337,8 +334,11 @@ def tile_scaleddotproductattention_pa_kernel(tc, q, k, v, mask, out):
 
         def add_row_sums(group):
             row_totals = stats.tile([P, GROUP], F32)
-            nc.vector.tensor_reduce(
-                out=row_totals[:], in_=row_sums[group][:], axis=mybir.AxisListType.X, op=ALU.add
+            nc.gpsimd.tensor_tensor(
+                out=row_totals[:],
+                in0=row_sums[group][:, :, 0],
+                in1=row_sums[group][:, :, 1],
+                op=ALU.add,
             )
             sums[group] = row_totals
 
@@ -398,16 +398,16 @@ def tile_scaleddotproductattention_pa_kernel(tc, q, k, v, mask, out):
                 divide_and_store((j - 3) // 2)
             if place == 1 and 0 <= head < HEADS:
                 quantise_v(head)
-            if 0 <= j < PAIRS and by_tensor(2 * j + 1):
-                first_half_maximum(2 * j + 1)
+            tensor_masked = 0 <= j < PAIRS and by_tensor(2 * j + 1)
             run(j, 0, row_maximum)
+            if tensor_masked:
+                half_maximum(2 * j + 1, 0)
+                half_maximum(2 * j + 1, 1)
+            elif 0 <= j < PAIRS:
+                row_maximum(2 * j + 1)
+
             if prepares:
                 take_q(nxt)
-            if 0 <= j < PAIRS:
-                if by_tensor(2 * j + 1):
-                    last_half_maximum(2 * j + 1)
-                else:
-                    row_maximum(2 * j + 1)
 
             run(j + 1, 0, mask_on_detour)
             run(j - 1, 0, regroup_e)
@@ -415,7 +415,6 @@ def tile_scaleddotproductattention_pa_kernel(tc, q, k, v, mask, out):
             if prepares:
                 take_k(nxt)
             run(j, 0, exponentials)
-            run(j, 1, exponentials)
             if 0 <= j + 2 < PAIRS and j % 2 == 0:
                 open_row_sums((j + 2) // 2)
             if place == 3 and 0 <= head < HEADS - 1:
@@ -438,6 +437,9 @@ def tile_scaleddotproductattention_pa_kernel(tc, q, k, v, mask, out):
                 mask_by_vector(2 * j + 3, 0)
                 mask_by_vector(2 * j + 3, 1)
             run(j + 2, 0, mask_by_vector, 0)
+            if tensor_masked:
+                combine_half_maxima(2 * j + 1)
+            run(j, 1, exponentials)
             if j % 2 == 0 and 0 <= (j - 1) // 2 < UNITS // GROUP and j >= 1:
                 add_row_sums((j - 1) // 2)
                 quantise_e((j - 1) // 2)

@@ -36,8 +36,7 @@ DETOUR_TILES = (0, 2, 4, 6)
 TICKS = 4
 VECTOR_BANKS = 2
 TENSOR_BANKS = 4
-E_BANKS = 2
-PV_WITH_E = True
+E_BANKS = 1
 
 
 def tile_scaleddotproductattention_pa_kernel(tc, q, k, v, mask, out):
@@ -58,8 +57,7 @@ def tile_scaleddotproductattention_pa_kernel(tc, q, k, v, mask, out):
         vector_psum = ctx.enter_context(tc.psum_pool(name="vector_psum", bufs=VECTOR_BANKS))
         tensor_psum = ctx.enter_context(tc.psum_pool(name="tensor_psum", bufs=TENSOR_BANKS))
         e_psum = ctx.enter_context(tc.psum_pool(name="e_psum", bufs=E_BANKS))
-        pv_psum = e_psum if PV_WITH_E else vector_psum
-        pv_tag = "e_bank" if PV_WITH_E else "vector_bank"
+        spare_psum = ctx.enter_context(tc.psum_pool(name="spare_psum", bufs=1))
 
         ident_bf16 = consts.tile([P, P], BF16)
         make_identity(nc, ident_bf16[:])
@@ -92,13 +90,15 @@ def tile_scaleddotproductattention_pa_kernel(tc, q, k, v, mask, out):
             nc.sync.dma_start(out=mask_sb[:, tile, :], in_=mask_tiles[0, :, tile, :])
 
         def transpose_blocks(rows):
-            t_bank = vector_psum.tile([P, TILES, P], BF16, tag="vector_bank")
+            t_bank = spare_psum.tile([P, TILES, P], BF16, tag="spare_bank")
             for block in range(TILES):
                 nc.tensor.transpose(t_bank[:, block, :], rows[:, block, :], ident_bf16[:])
             return t_bank
 
-        def transpose_q_k(head):
+        def transpose_q(head):
             q_banks[head] = transpose_blocks(q_rows[head])
+
+        def transpose_k(head):
             k_banks[head] = transpose_blocks(k_rows[head])
 
         def take_q(head):
@@ -295,7 +295,7 @@ def tile_scaleddotproductattention_pa_kernel(tc, q, k, v, mask, out):
 
         def regroup_e(unit):
             group, member = divmod(unit, GROUP)
-            if member == 0:
+            if group not in e_grouped:
                 grouped = groups.tile([P, GROUP, PASSES, P, PACK], BF16, align_bytes=64)
                 e_grouped[group] = grouped
             nc.scalar.copy(
@@ -318,7 +318,7 @@ def tile_scaleddotproductattention_pa_kernel(tc, q, k, v, mask, out):
         def multiply_e_v(group):
             head = group * GROUP // TILES
             codes, scale_plane = e_codes[group], e_scales[group]
-            pv_bank = pv_psum.tile([P, GROUP, D], F32, tag=pv_tag)
+            pv_bank = spare_psum.tile([P, GROUP, D], F32, tag="spare_bank")
             for member in range(GROUP):
                 for g in range(PASSES):
                     nc.tensor.matmul_mx(
@@ -360,87 +360,86 @@ def tile_scaleddotproductattention_pa_kernel(tc, q, k, v, mask, out):
                 out=out_heads[head][:, first_tile : first_tile + GROUP, :], in_=out_sb[:]
             )
 
-        def ends_head_at(pair, offset):
-            head, rest = divmod(pair - offset, TILES // 2)
-            return head if rest == 0 and 0 <= head < HEADS else None
+        PAIRS = UNITS // 2
+        PAIRS_A_HEAD = TILES // 2
+
+        def at(pair, member, stage, *args):
+            if 0 <= pair < PAIRS:
+                stage(2 * pair + member, *args)
 
         ctx.enter_context(tc.manual_schedule())
         load_head(0)
         load_mask(0)
         load_mask(1)
         load_v(0)
+        load_head(1)
         for tile in range(2, TILES):
             load_mask(tile)
-        load_head(1)
         load_v(1)
-        transpose_q_k(0)
+        transpose_q(0)
         take_q(0)
+        transpose_k(0)
         take_k(0)
         regroup_v(0)
 
-        PAIRS = UNITS // 2
+        for j in range(-2, PAIRS + 5):
+            head, place = divmod(j, PAIRS_A_HEAD)
+            odd_cycle = j % 2 == 1
+            by_t = 0 <= j < PAIRS and by_tensor(2 * j + 1)
+            q_head = (j + 5) // 4 if j >= 3 and (j + 5) % 4 == 0 else (1 if j == 0 else None)
+            k_head = (j + 3) // 4 if j >= 1 and (j + 3) % 4 == 0 else None
+            q_head = q_head if q_head is not None and q_head < HEADS else None
+            k_head = k_head if k_head is not None and k_head < HEADS else None
 
-        def run(pairs, unit_of_pair, stage, *args):
-            if 0 <= pairs < PAIRS:
-                stage(2 * pairs + unit_of_pair, *args)
-
-        for j in range(-2, PAIRS + 4):
-            head, place = divmod(j, TILES // 2)
-            group = (j - 1) // 2
-            nxt = head + 1
-            prepares = place == 2 and 1 <= nxt < HEADS
-
-            run(j - 1, 1, transpose_e)
-            if prepares:
-                transpose_q_k(nxt)
-
-            if j % 2 == 0 and 0 <= (j - 3) // 2 < UNITS // GROUP and j >= 3:
-                divide_and_store((j - 3) // 2)
-            if place == 1 and 0 <= head < HEADS:
-                quantise_v(head)
-            tensor_masked = 0 <= j < PAIRS and by_tensor(2 * j + 1)
-            run(j, 0, row_maximum)
-            if tensor_masked:
+            if odd_cycle and 0 <= (j - 3) // 2 < UNITS // GROUP:
+                add_row_sums((j - 3) // 2)
+            at(j + 1, 0, mask_by_vector, 0)
+            at(j - 2, 0, transpose_e)
+            if not odd_cycle and 0 <= (j - 4) // 2 < UNITS // GROUP:
+                multiply_e_v((j - 4) // 2)
+            if q_head is not None:
+                transpose_q(q_head)
+            if k_head is not None:
+                transpose_k(k_head)
+            if by_t:
                 half_maximum(2 * j + 1, 0)
                 half_maximum(2 * j + 1, 1)
             elif 0 <= j < PAIRS:
+                mask_by_vector(2 * j + 1, 0)
+                mask_by_vector(2 * j + 1, 1)
+            at(j + 1, 0, mask_on_detour)
+            at(j + 1, 1, scores_for_tensor)
+            at(j - 2, 0, regroup_e)
+            at(j, 0, row_maximum)
+            at(j + 2, 0, scores_for_vector)
+            at(j - 1, 0, exponentials)
+            at(j - 1, 1, transpose_e)
+            if by_t:
+                combine_half_maxima(2 * j + 1)
+            elif 0 <= j < PAIRS:
                 row_maximum(2 * j + 1)
+            if q_head is not None:
+                take_q(q_head)
+            if odd_cycle and 0 <= (j - 3) // 2 < UNITS // GROUP:
+                quantise_e((j - 3) // 2)
+                invert((j - 3) // 2)
+            if not odd_cycle and 0 <= (j - 4) // 2 < UNITS // GROUP:
+                divide_and_store((j - 4) // 2)
+            if place == 2 and 0 <= head < HEADS:
+                quantise_v(head)
+            if 0 <= j + 1 < PAIRS and by_tensor(2 * j + 3):
+                mask_by_tensor(2 * j + 3)
+            at(j - 1, 1, regroup_e)
+            if k_head is not None:
+                take_k(k_head)
+            at(j, 1, exponentials)
 
-            if prepares:
-                take_q(nxt)
-
-            run(j + 1, 0, mask_on_detour)
-            run(j - 1, 0, regroup_e)
-            run(j - 1, 1, regroup_e)
-            if prepares:
-                take_k(nxt)
-            run(j, 0, exponentials)
-            if 0 <= j + 2 < PAIRS and j % 2 == 0:
-                open_row_sums((j + 2) // 2)
-            if place == 3 and 0 <= head < HEADS - 1:
-                regroup_v(head + 1)
+            if odd_cycle and 0 <= (j + 1) // 2 < UNITS // GROUP:
+                open_row_sums((j + 1) // 2)
+            if place == 0 and 1 <= head < HEADS:
+                regroup_v(head)
             if 0 <= j < len(TENSOR_TILES):
                 make_tables(j)
             if place == 0 and 0 <= head < HEADS - 2:
                 load_head(head + 2)
                 load_v(head + 2)
-
-            run(j + 1, 1, scores_for_tensor)
-            if j % 2 == 1 and 0 <= (j - 2) // 2 < UNITS // GROUP:
-                multiply_e_v((j - 2) // 2)
-            run(j + 2, 0, scores_for_vector)
-            if 0 <= j + 1 < PAIRS and by_tensor(2 * j + 3):
-                mask_by_tensor(2 * j + 3)
-            run(j, 0, transpose_e)
-
-            if 0 <= j + 1 < PAIRS and not by_tensor(2 * j + 3):
-                mask_by_vector(2 * j + 3, 0)
-                mask_by_vector(2 * j + 3, 1)
-            run(j + 2, 0, mask_by_vector, 0)
-            if tensor_masked:
-                combine_half_maxima(2 * j + 1)
-            run(j, 1, exponentials)
-            if j % 2 == 0 and 0 <= (j - 1) // 2 < UNITS // GROUP and j >= 1:
-                add_row_sums((j - 1) // 2)
-                quantise_e((j - 1) // 2)
-                invert((j - 1) // 2)

@@ -31,8 +31,8 @@ FLOPS = 2 * 2 * HEADS * S * S * D
 
 TENSOR_TILES = (1, 3, 5, 7)
 BIG = 2.0**120
-FIRST_TENSOR_HEAD = 1
-DETOUR_TILES = (0, 2, 4, 6)
+FIRST_TENSOR_UNIT = 3
+DETOUR_TILES = (0, 2, 6)
 TICKS = 4
 VECTOR_BANKS = 2
 TENSOR_BANKS = 4
@@ -89,8 +89,8 @@ def tile_scaleddotproductattention_pa_kernel(tc, q, k, v, mask, out):
         def load_mask(tile):
             nc.sync.dma_start(out=mask_sb[:, tile, :], in_=mask_tiles[0, :, tile, :])
 
-        def transpose_blocks(rows):
-            t_bank = spare_psum.tile([P, TILES, P], BF16, tag="spare_bank")
+        def transpose_blocks(rows, pool=None, tag="spare_bank"):
+            t_bank = (pool or spare_psum).tile([P, TILES, P], BF16, tag=tag)
             for block in range(TILES):
                 nc.tensor.transpose(t_bank[:, block, :], rows[:, block, :], ident_bf16[:])
             return t_bank
@@ -99,7 +99,10 @@ def tile_scaleddotproductattention_pa_kernel(tc, q, k, v, mask, out):
             q_banks[head] = transpose_blocks(q_rows[head])
 
         def transpose_k(head):
-            k_banks[head] = transpose_blocks(k_rows[head])
+            if head == 0:
+                k_banks[head] = transpose_blocks(k_rows[head], tensor_psum, "tensor_bank")
+            else:
+                k_banks[head] = transpose_blocks(k_rows[head])
 
         def take_q(head):
             q_cols = heads.tile([P, TILES, P], BF16)
@@ -119,7 +122,7 @@ def tile_scaleddotproductattention_pa_kernel(tc, q, k, v, mask, out):
 
         def make_tables(index):
             mask_rows = mask_sb[:, TENSOR_TILES[index], :].rearrange("p (t k) -> p t k", k=P)
-            t_bank = transpose_blocks(mask_rows)
+            t_bank = transpose_blocks(mask_rows, e_psum, "e_bank")
             mask_t = heads.tile([P, TILES, P], BF16)
             nc.scalar.copy(out=mask_t[:], in_=t_bank[:])
             for table, big in ((plus_big, BIG), (minus_big, -BIG)):
@@ -156,10 +159,10 @@ def tile_scaleddotproductattention_pa_kernel(tc, q, k, v, mask, out):
 
         def by_tensor(unit):
             head, tile = divmod(unit, TILES)
-            return head >= FIRST_TENSOR_HEAD and tile in TENSOR_TILES
+            return unit >= FIRST_TENSOR_UNIT and tile in TENSOR_TILES
 
         def takes_detour(unit):
-            return unit % TILES in DETOUR_TILES
+            return unit > 2 and unit % TILES in DETOUR_TILES
 
         def multiply_q_k(unit, half, bank, stop):
             head, tile = divmod(unit, TILES)
@@ -284,7 +287,10 @@ def tile_scaleddotproductattention_pa_kernel(tc, q, k, v, mask, out):
 
         def transpose_e(unit):
             e_words = e_rows[unit][:].bitcast(F32)
-            e_words_t = e_psum.tile([P, PASSES, PAIR, P], F32, tag="e_bank")
+            if unit < UNITS - 2:
+                e_words_t = e_psum.tile([P, PASSES, PAIR, P], F32, tag="e_bank")
+            else:
+                e_words_t = tensor_psum.tile([P, PASSES, PAIR, P], F32, tag="tensor_bank")
             for u in range(PAIR):
                 for g in range(PASSES):
                     first = (g * PAIR + u if by_tensor(unit) else u * PASSES + g) * P
@@ -293,36 +299,40 @@ def tile_scaleddotproductattention_pa_kernel(tc, q, k, v, mask, out):
                     )
             e_t[unit] = e_words_t
 
-        def regroup_e(unit):
+        def regroup_e(unit, by_vector=False):
             group, member = divmod(unit, GROUP)
             if group not in e_grouped:
                 grouped = groups.tile([P, GROUP, PASSES, P, PACK], BF16, align_bytes=64)
                 e_grouped[group] = grouped
-            nc.scalar.copy(
+            (nc.vector.tensor_copy if by_vector else nc.scalar.copy)(
                 out=e_grouped[group][:, member].bitcast(F32),
                 in_=e_t[unit][:].rearrange("p g u n -> p g n u"),
             )
 
-        def quantise_e(group):
-            codes = groups.tile([P, GROUP, PASSES, P], U32, align_bytes=64, name="e_code_words")
-            scale_plane = groups.tile(
-                [P, GROUP, PASSES, P], U8, align_bytes=64, name="e_scale_plane"
-            )
+        def quantise_e(group, first=0, count=GROUP):
+            if first == 0:
+                codes = groups.tile([P, GROUP, PASSES, P], U32, align_bytes=64, name="e_code_words")
+                scale_plane = groups.tile(
+                    [P, GROUP, PASSES, P], U8, align_bytes=64, name="e_scale_plane"
+                )
+                e_codes[group], e_scales[group] = codes, scale_plane
+            members = slice(first, first + count)
             nc.vector.quantize_mx(
-                out=codes[:].rearrange("p m g n -> p (m g n)").bitcast(FP8X4),
-                scales=scale_plane[:].rearrange("p m g n -> p (m g n)"),
-                in_=e_grouped[group][:].rearrange("p m g n t -> p (m g n t)"),
+                out=e_codes[group][:, members].rearrange("p m g n -> p (m g n)").bitcast(FP8X4),
+                scales=e_scales[group][:, members].rearrange("p m g n -> p (m g n)"),
+                in_=e_grouped[group][:, members].rearrange("p m g n t -> p (m g n t)"),
             )
-            e_codes[group], e_scales[group] = codes, scale_plane
 
-        def multiply_e_v(group):
+        def multiply_e_v(group, first=0, count=GROUP):
             head = group * GROUP // TILES
             codes, scale_plane = e_codes[group], e_scales[group]
-            pv_bank = spare_psum.tile([P, GROUP, D], F32, tag="spare_bank")
-            for member in range(GROUP):
+            if first == 0:
+                pv_bank = spare_psum.tile([P, GROUP, D], F32, tag="spare_bank")
+                pv[group] = pv_bank
+            for member in range(first, first + count):
                 for g in range(PASSES):
                     nc.tensor.matmul_mx(
-                        out=pv_bank[:, member, :],
+                        out=pv[group][:, member, :],
                         lhsT=codes[:, member, g, :].bitcast(FP8X4),
                         lhsT_scale=scale_plane[:, member, g, :],
                         rhs=v_codes[head][:, g, :].bitcast(FP8X4),
@@ -330,7 +340,6 @@ def tile_scaleddotproductattention_pa_kernel(tc, q, k, v, mask, out):
                         start=(g == 0),
                         stop=(g == PASSES - 1),
                     )
-            pv[group] = pv_bank
 
         def add_row_sums(group):
             row_totals = stats.tile([P, GROUP], F32)
@@ -369,20 +378,21 @@ def tile_scaleddotproductattention_pa_kernel(tc, q, k, v, mask, out):
 
         ctx.enter_context(tc.manual_schedule())
         load_head(0)
-        load_mask(0)
-        load_mask(1)
-        load_v(0)
-        load_head(1)
-        for tile in range(2, TILES):
+        for tile in (0, 3, 1, 2, 5):
             load_mask(tile)
+        load_v(0)
+        load_mask(7)
+        load_head(1)
+        load_mask(4)
+        load_mask(6)
         load_v(1)
+        open_row_sums(0)
         transpose_q(0)
         take_q(0)
         transpose_k(0)
         take_k(0)
-        regroup_v(0)
 
-        for j in range(-2, PAIRS + 5):
+        for j in range(-2, PAIRS):
             head, place = divmod(j, PAIRS_A_HEAD)
             odd_cycle = j % 2 == 1
             by_t = 0 <= j < PAIRS and by_tensor(2 * j + 1)
@@ -394,6 +404,8 @@ def tile_scaleddotproductattention_pa_kernel(tc, q, k, v, mask, out):
             if odd_cycle and 0 <= (j - 3) // 2 < UNITS // GROUP:
                 add_row_sums((j - 3) // 2)
             at(j + 1, 0, mask_by_vector, 0)
+            if 0 <= j + 1 < PAIRS and not takes_detour(2 * j + 2):
+                mask_by_vector(2 * j + 2, 1)
             at(j - 2, 0, transpose_e)
             if not odd_cycle and 0 <= (j - 4) // 2 < UNITS // GROUP:
                 multiply_e_v((j - 4) // 2)
@@ -407,12 +419,15 @@ def tile_scaleddotproductattention_pa_kernel(tc, q, k, v, mask, out):
             elif 0 <= j < PAIRS:
                 mask_by_vector(2 * j + 1, 0)
                 mask_by_vector(2 * j + 1, 1)
-            at(j + 1, 0, mask_on_detour)
+            if 0 <= j + 1 < PAIRS and takes_detour(2 * j + 2):
+                mask_on_detour(2 * j + 2)
             at(j + 1, 1, scores_for_tensor)
             at(j - 2, 0, regroup_e)
-            at(j, 0, row_maximum)
+            if j > 0:
+                row_maximum(2 * j)
             at(j + 2, 0, scores_for_vector)
-            at(j - 1, 0, exponentials)
+            if j - 1 > 0:
+                exponentials(2 * j - 2)
             at(j - 1, 1, transpose_e)
             if by_t:
                 combine_half_maxima(2 * j + 1)
@@ -432,14 +447,38 @@ def tile_scaleddotproductattention_pa_kernel(tc, q, k, v, mask, out):
             at(j - 1, 1, regroup_e)
             if k_head is not None:
                 take_k(k_head)
+            if j == PAIRS - 1:
+                exponentials(2 * j)
             at(j, 1, exponentials)
 
-            if odd_cycle and 0 <= (j + 1) // 2 < UNITS // GROUP:
+            if odd_cycle and 0 < (j + 1) // 2 < UNITS // GROUP:
                 open_row_sums((j + 1) // 2)
-            if place == 0 and 1 <= head < HEADS:
+            if j == -1:
+                row_maximum(0)
+            if place == 0 and 0 <= head < HEADS:
                 regroup_v(head)
-            if 0 <= j < len(TENSOR_TILES):
-                make_tables(j)
+            for index, cycle in ((1, -2), (2, -1), (3, -1), (0, 0)):
+                if j == cycle:
+                    make_tables(index)
+                    if index == 2:
+                        exponentials(0)
             if place == 0 and 0 <= head < HEADS - 2:
                 load_head(head + 2)
                 load_v(head + 2)
+
+        last = UNITS // GROUP - 1
+        transpose_e(UNITS - 4)
+        multiply_e_v(last - 1)
+        transpose_e(UNITS - 2)
+        regroup_e(UNITS - 4, by_vector=True)
+        regroup_e(UNITS - 2)
+        divide_and_store(last - 1)
+        quantise_e(last, 0, 2)
+        transpose_e(UNITS - 1)
+        regroup_e(UNITS - 1)
+        add_row_sums(last)
+        invert(last)
+        multiply_e_v(last, 0, 2)
+        quantise_e(last, 2, 2)
+        multiply_e_v(last, 2, 2)
+        divide_and_store(last)

@@ -75,11 +75,41 @@ def tile_scaleddotproductattention_pa_kernel(tc, q, k, v, mask, out):
         sums = {}
 
         def load_head(head):
-            q_in = heads.tile([P, TILES, D], BF16)
+            q_in = heads.tile([P, TILES, D], BF16, tag="q_in")
             nc.sync.dma_start(out=q_in[:], in_=q_heads[head])
-            k_in = heads.tile([P, TILES, D], BF16)
+            k_in = heads.tile([P, TILES, D], BF16, tag="k_in")
             nc.sync.dma_start(out=k_in[:], in_=k_heads[head])
             q_rows[head], k_rows[head] = q_in, k_in
+
+        def load_first_head():
+            q_in = heads.tile([P, TILES, D], BF16, tag="q_in")
+            k_in = heads.tile([P, TILES, D], BF16, tag="k_in")
+            nc.sync.dma_start(out=k_in[:, 0:4], in_=k_heads[0][:, 0:4])
+            nc.sync.dma_start(out=q_in[:, 0:2], in_=q_heads[0][:, 0:2])
+            nc.sync.dma_start(out=k_in[:, 4:8], in_=k_heads[0][:, 4:8])
+            nc.sync.dma_start(out=q_in[:, 2:8], in_=q_heads[0][:, 2:8])
+            q_rows[0], k_rows[0] = q_in, k_in
+
+        def transpose_first_head():
+            q_cols = heads.tile([P, TILES, P], BF16, tag="q_cols")
+            k_cols = heads.tile([P, TILES, P], BF16, tag="k_cols")
+            for rows, cols, first, end, pool, tag, by_vector in (
+                (k_rows[0], k_cols, 0, 4, tensor_psum, "tensor_bank", False),
+                (q_rows[0], q_cols, 0, 2, spare_psum, "spare_bank", True),
+                (k_rows[0], k_cols, 4, 8, tensor_psum, "tensor_bank", False),
+                (q_rows[0], q_cols, 2, 8, e_psum, "e_bank", True),
+            ):
+                t_bank = pool.tile([P, TILES, P], BF16, tag=tag)
+                for block in range(first, end):
+                    nc.tensor.transpose(t_bank[:, block, :], rows[:, block, :], ident_bf16[:])
+                if by_vector:
+                    nc.vector.tensor_scalar(
+                        out=cols[:, first:end], in0=t_bank[:, first:end], scalar1=1.0 / TEMPERATURE,
+                        scalar2=None, op0=ALU.mult,
+                    )
+                else:
+                    nc.scalar.copy(out=cols[:, first:end], in_=t_bank[:, first:end])
+            q_t[0], k_t[0] = q_cols, k_cols
 
         def load_v(head):
             v_in = heads.tile([P, PASSES, PACK, D], BF16)
@@ -99,13 +129,10 @@ def tile_scaleddotproductattention_pa_kernel(tc, q, k, v, mask, out):
             q_banks[head] = transpose_blocks(q_rows[head])
 
         def transpose_k(head):
-            if head == 0:
-                k_banks[head] = transpose_blocks(k_rows[head], tensor_psum, "tensor_bank")
-            else:
-                k_banks[head] = transpose_blocks(k_rows[head])
+            k_banks[head] = transpose_blocks(k_rows[head])
 
         def take_q(head):
-            q_cols = heads.tile([P, TILES, P], BF16)
+            q_cols = heads.tile([P, TILES, P], BF16, tag="q_cols")
             nc.vector.tensor_scalar(
                 out=q_cols[:],
                 in0=q_banks[head][:],
@@ -116,7 +143,7 @@ def tile_scaleddotproductattention_pa_kernel(tc, q, k, v, mask, out):
             q_t[head] = q_cols
 
         def take_k(head):
-            k_cols = heads.tile([P, TILES, P], BF16)
+            k_cols = heads.tile([P, TILES, P], BF16, tag="k_cols")
             nc.scalar.copy(out=k_cols[:], in_=k_banks[head][:])
             k_t[head] = k_cols
 
@@ -356,17 +383,17 @@ def tile_scaleddotproductattention_pa_kernel(tc, q, k, v, mask, out):
             nc.vector.reciprocal(out=inverse[:], in_=sums[group][:])
             row_sums[group] = inverse
 
-        def divide_and_store(group):
-            head, first_tile = divmod(group * GROUP, TILES)
-            out_sb = groups.tile([P, GROUP, D], F32)
+        def divide_and_store(group, first=0, count=GROUP):
+            head, first_tile = divmod(group * GROUP + first, TILES)
+            out_sb = groups.tile([P, count, D], F32, tag="out_sb" if count == GROUP else "out_part")
             nc.vector.tensor_tensor(
                 out=out_sb[:],
-                in0=pv[group][:],
-                in1=row_sums[group][:].unsqueeze(2).to_broadcast([P, GROUP, D]),
+                in0=pv[group][:, first : first + count],
+                in1=row_sums[group][:, first : first + count].unsqueeze(2).to_broadcast([P, count, D]),
                 op=ALU.mult,
             )
             nc.sync.dma_start(
-                out=out_heads[head][:, first_tile : first_tile + GROUP, :], in_=out_sb[:]
+                out=out_heads[head][:, first_tile : first_tile + count, :], in_=out_sb[:]
             )
 
         PAIRS = UNITS // 2
@@ -377,7 +404,7 @@ def tile_scaleddotproductattention_pa_kernel(tc, q, k, v, mask, out):
                 stage(2 * pair + member, *args)
 
         ctx.enter_context(tc.manual_schedule())
-        load_head(0)
+        load_first_head()
         for tile in (0, 3, 1, 2, 5):
             load_mask(tile)
         load_v(0)
@@ -387,10 +414,7 @@ def tile_scaleddotproductattention_pa_kernel(tc, q, k, v, mask, out):
         load_mask(6)
         load_v(1)
         open_row_sums(0)
-        transpose_q(0)
-        take_q(0)
-        transpose_k(0)
-        take_k(0)
+        transpose_first_head()
 
         for j in range(-2, PAIRS):
             head, place = divmod(j, PAIRS_A_HEAD)
@@ -423,6 +447,8 @@ def tile_scaleddotproductattention_pa_kernel(tc, q, k, v, mask, out):
                 mask_on_detour(2 * j + 2)
             at(j + 1, 1, scores_for_tensor)
             at(j - 2, 0, regroup_e)
+            if k_head is not None:
+                take_k(k_head)
             if j > 0:
                 row_maximum(2 * j)
             at(j + 2, 0, scores_for_vector)
@@ -445,8 +471,6 @@ def tile_scaleddotproductattention_pa_kernel(tc, q, k, v, mask, out):
             if 0 <= j + 1 < PAIRS and by_tensor(2 * j + 3):
                 mask_by_tensor(2 * j + 3)
             at(j - 1, 1, regroup_e)
-            if k_head is not None:
-                take_k(k_head)
             if j == PAIRS - 1:
                 exponentials(2 * j)
             at(j, 1, exponentials)
@@ -479,6 +503,9 @@ def tile_scaleddotproductattention_pa_kernel(tc, q, k, v, mask, out):
         add_row_sums(last)
         invert(last)
         multiply_e_v(last, 0, 2)
-        quantise_e(last, 2, 2)
-        multiply_e_v(last, 2, 2)
-        divide_and_store(last)
+        quantise_e(last, 2, 1)
+        multiply_e_v(last, 2, 1)
+        quantise_e(last, 3, 1)
+        multiply_e_v(last, 3, 1)
+        divide_and_store(last, 0, 3)
+        divide_and_store(last, 3, 1)

from contextlib import ExitStack

import concourse.mybir as mybir
from concourse.masks import make_identity

BF16 = mybir.dt.bfloat16
F32 = mybir.dt.float32
U32 = mybir.dt.uint32
U8 = mybir.dt.uint8
FP8X4 = mybir.dt.float8_e4m3fn_x4
ALU = mybir.AluOpType
ACT = mybir.ActivationFunctionType

P = 128
HEADS = 16
S = 1024
D = 128
TEMPERATURE = 8.0
TILES = S // P
UNITS = HEADS * TILES
GROUP = 4
BANK = 512
HALVES = S // BANK
PACK = 4
K_PASS = P * PACK
PASSES = S // K_PASS
PAIR = 2
WORD_BLOCKS = S // (PAIR * P)

FLOPS = 2 * 2 * HEADS * S * S * D

TENSOR_TILES = (1, 3, 5, 7)
BIG = 2.0**120
FIRST_TENSOR_UNIT = 3
DETOUR_TILES = (0, 2, 6)
TICKS = 4
VECTOR_BANKS = 2
TENSOR_BANKS = 4
E_BANKS = 1


def tile_scaleddotproductattention_pa_kernel(tc, q, k, v, mask, out):
    nc = tc.nc

    q_heads = q.rearrange("b h (p t) d -> (b h) p t d", t=TILES)
    k_heads = k.rearrange("b h (t p) d -> (b h) p t d", p=P)
    mask_tiles = mask.rearrange("a b (p t) k -> (a b) p t k", t=TILES)
    out_heads = out.rearrange("b h (p t) d -> (b h) p t d", t=TILES)
    v_heads = v.rearrange("b h (g p n) d -> (b h) p g n d", p=P, n=PACK)

    with ExitStack() as ctx:
        consts = ctx.enter_context(tc.tile_pool(name="consts", bufs=1))
        heads = ctx.enter_context(tc.tile_pool(name="heads", bufs=3))
        groups = ctx.enter_context(tc.tile_pool(name="groups", bufs=3))
        units = ctx.enter_context(tc.tile_pool(name="units", bufs=4))
        stats = ctx.enter_context(tc.tile_pool(name="stats", bufs=8))
        vector_psum = ctx.enter_context(tc.psum_pool(name="vector_psum", bufs=VECTOR_BANKS))
        tensor_psum = ctx.enter_context(tc.psum_pool(name="tensor_psum", bufs=TENSOR_BANKS))
        e_psum = ctx.enter_context(tc.psum_pool(name="e_psum", bufs=E_BANKS))
        spare_psum = ctx.enter_context(tc.psum_pool(name="spare_psum", bufs=1))

        ident_bf16 = consts.tile([P, P], BF16)
        make_identity(nc, ident_bf16[:])
        ident_f32 = consts.tile([P, P], F32)
        make_identity(nc, ident_f32[:])
        mask_sb = consts.tile([P, TILES, S], BF16)
        plus_big = consts.tile([P, len(TENSOR_TILES), TILES, P], F32)
        minus_big = consts.tile([P, len(TENSOR_TILES), TILES, P], F32)

        q_rows, k_rows, v_rows, v_grouped = {}, {}, {}, {}
        q_banks, k_banks, q_t, k_t, v_codes, v_scales = {}, {}, {}, {}, {}, {}
        e_grouped, e_codes, e_scales, row_sums, pv = {}, {}, {}, {}, {}
        scores, masked, neg_max, e_rows, e_t = {}, {}, {}, {}, {}
        half_maxima = {}
        sums = {}

        def load_head(head):
            q_in = heads.tile([P, TILES, D], BF16, tag="q_in")
            nc.sync.dma_start(out=q_in[:], in_=q_heads[head])
            k_in = heads.tile([P, TILES, D], BF16, tag="k_in")
            nc.sync.dma_start(out=k_in[:], in_=k_heads[head])
            q_rows[head], k_rows[head] = q_in, k_in

        def load_first_head():
            q_in = heads.tile([P, TILES, D], BF16, tag="q_in")
            k_in = heads.tile([P, TILES, D], BF16, tag="k_in")
            nc.sync.dma_start(out=k_in[:, 0:4], in_=k_heads[0][:, 0:4])
            nc.sync.dma_start(out=q_in[:, 0:2], in_=q_heads[0][:, 0:2])
            nc.sync.dma_start(out=k_in[:, 4:8], in_=k_heads[0][:, 4:8])
            nc.sync.dma_start(out=q_in[:, 2:8], in_=q_heads[0][:, 2:8])
            q_rows[0], k_rows[0] = q_in, k_in

        def transpose_first_head():
            q_cols = heads.tile([P, TILES, P], BF16, tag="q_cols")
            k_cols = heads.tile([P, TILES, P], BF16, tag="k_cols")
            for rows, cols, first, end, pool, tag, by_vector in (
                (k_rows[0], k_cols, 0, 4, tensor_psum, "tensor_bank", False),
                (q_rows[0], q_cols, 0, 2, spare_psum, "spare_bank", True),
                (k_rows[0], k_cols, 4, 8, tensor_psum, "tensor_bank", False),
                (q_rows[0], q_cols, 2, 8, e_psum, "e_bank", True),
            ):
                t_bank = pool.tile([P, TILES, P], BF16, tag=tag)
                for block in range(first, end):
                    nc.tensor.transpose(t_bank[:, block, :], rows[:, block, :], ident_bf16[:])
                if by_vector:
                    nc.vector.tensor_scalar(
                        out=cols[:, first:end], in0=t_bank[:, first:end], scalar1=1.0 / TEMPERATURE,
                        scalar2=None, op0=ALU.mult,
                    )
                else:
                    nc.scalar.copy(out=cols[:, first:end], in_=t_bank[:, first:end])
            q_t[0], k_t[0] = q_cols, k_cols

        def load_v(head):
            v_in = heads.tile([P, PASSES, PACK, D], BF16)
            nc.sync.dma_start(out=v_in[:], in_=v_heads[head])
            v_rows[head] = v_in

        def load_mask(tile):
            nc.sync.dma_start(out=mask_sb[:, tile, :], in_=mask_tiles[0, :, tile, :])

        def transpose_blocks(rows, pool=None, tag="spare_bank"):
            t_bank = (pool or spare_psum).tile([P, TILES, P], BF16, tag=tag)
            for block in range(TILES):
                nc.tensor.transpose(t_bank[:, block, :], rows[:, block, :], ident_bf16[:])
            return t_bank

        def transpose_q(head):
            q_banks[head] = transpose_blocks(q_rows[head])

        def transpose_k(head):
            k_banks[head] = transpose_blocks(k_rows[head])

        def take_q(head):
            q_cols = heads.tile([P, TILES, P], BF16, tag="q_cols")
            nc.vector.tensor_scalar(
                out=q_cols[:],
                in0=q_banks[head][:],
                scalar1=1.0 / TEMPERATURE,
                scalar2=None,
                op0=ALU.mult,
            )
            q_t[head] = q_cols

        def take_k(head):
            k_cols = heads.tile([P, TILES, P], BF16, tag="k_cols")
            nc.scalar.copy(out=k_cols[:], in_=k_banks[head][:])
            k_t[head] = k_cols

        def make_tables(index):
            mask_rows = mask_sb[:, TENSOR_TILES[index], :].rearrange("p (t k) -> p t k", k=P)
            t_bank = transpose_blocks(mask_rows, e_psum, "e_bank")
            mask_t = heads.tile([P, TILES, P], BF16)
            nc.scalar.copy(out=mask_t[:], in_=t_bank[:])
            for table, big in ((plus_big, BIG), (minus_big, -BIG)):
                nc.gpsimd.tensor_scalar(
                    out=table[:, index],
                    in0=mask_t[:],
                    scalar1=-big,
                    scalar2=big,
                    op0=ALU.mult,
                    op1=ALU.add,
                )

        def regroup_v(head):
            grouped = consts.tile([P, PASSES, D, PACK], BF16, align_bytes=64, name="v_grouped_keys")
            nc.gpsimd.tensor_scalar(
                out=grouped[:],
                in0=v_rows[head][:].rearrange("p g n d -> p g d n"),
                scalar1=1.0,
                scalar2=0.0,
                op0=ALU.mult,
                op1=ALU.add,
            )
            v_grouped[head] = grouped

        def quantise_v(head):
            codes = heads.tile([P, PASSES, D], U32, align_bytes=64, name="v_code_words")
            scale_plane = heads.tile([P, PASSES, D], U8, align_bytes=64, name="v_scale_plane")
            nc.vector.quantize_mx(
                out=codes[:].rearrange("p g d -> p (g d)").bitcast(FP8X4),
                scales=scale_plane[:].rearrange("p g d -> p (g d)"),
                in_=v_grouped[head][:].rearrange("p g d n -> p (g d n)"),
            )
            v_codes[head], v_scales[head] = codes, scale_plane

        def by_tensor(unit):
            head, tile = divmod(unit, TILES)
            return unit >= FIRST_TENSOR_UNIT and tile in TENSOR_TILES

        def takes_detour(unit):
            return unit > 2 and unit % TILES in DETOUR_TILES

        def multiply_q_k(unit, half, bank, stop):
            head, tile = divmod(unit, TILES)
            key_tiles = slice(half * BANK // P, (half + 1) * BANK // P)
            nc.tensor.matmul(
                out=bank,
                lhsT=q_t[head][:, tile, :],
                rhs=k_t[head][:, key_tiles, :].rearrange("d t p -> d (t p)"),
                start=True,
                stop=stop,
            )

        def scores_for_vector(unit):
            for half in range(HALVES):
                score_bank = vector_psum.tile([P, BANK], F32, tag="vector_bank")
                multiply_q_k(unit, half, score_bank[:], True)
                scores[unit, half] = score_bank
            masked_rows = units.tile([P, S], F32)
            masked[unit] = masked_rows

        def scores_for_tensor(unit):
            for half in range(HALVES):
                score_bank = tensor_psum.tile([P, BANK], F32, tag="tensor_bank")
                multiply_q_k(unit, half, score_bank[:], not by_tensor(unit))
                scores[unit, half] = score_bank
            if not by_tensor(unit):
                masked_rows = units.tile([P, S], F32)
                masked[unit] = masked_rows

        def mask_by_tensor(unit):
            index = TENSOR_TILES.index(unit % TILES)
            for half in range(HALVES):
                for table in (plus_big, minus_big):
                    for t in range(BANK // P):
                        nc.tensor.matmul(
                            out=scores[unit, half][:, t * P : (t + 1) * P],
                            lhsT=table[:, index, half * BANK // P + t, :],
                            rhs=ident_f32[:],
                            start=False,
                            stop=(table is minus_big and t == BANK // P - 1),
                            is_transpose=True,
                        )

        def mask_by_vector(unit, half):
            keys = slice(half * BANK, (half + 1) * BANK)
            nc.vector.tensor_tensor(
                out=masked[unit][:, keys],
                in0=scores[unit, half][:],
                in1=mask_sb[:, unit % TILES, keys],
                op=ALU.mult,
            )

        def mask_on_detour(unit):
            keys = slice((HALVES - 1) * BANK, S)
            unmasked = units.tile([P, BANK], F32)
            nc.scalar.copy(out=unmasked[:], in_=scores[unit, HALVES - 1][:])
            nc.gpsimd.tensor_tensor(
                out=masked[unit][:, keys],
                in0=unmasked[:],
                in1=mask_sb[:, unit % TILES, keys],
                op=ALU.mult,
            )

        def row_maximum(unit):
            minus_max = stats.tile([P, 1], F32)
            nc.vector.tensor_reduce(
                out=minus_max[:],
                in_=masked[unit][:],
                axis=mybir.AxisListType.X,
                op=ALU.max,
                negate=True,
            )
            neg_max[unit] = minus_max

        def half_maximum(unit, half):
            if half == 0:
                maxima = stats.tile([P, HALVES], F32)
                half_maxima[unit] = maxima
            nc.vector.tensor_reduce(
                out=half_maxima[unit][:, half : half + 1],
                in_=scores[unit, half][:],
                axis=mybir.AxisListType.X,
                op=ALU.max,
                negate=True,
            )

        def combine_half_maxima(unit):
            minus_max = stats.tile([P, 1], F32)
            nc.vector.tensor_reduce(
                out=minus_max[:],
                in_=half_maxima[unit][:],
                axis=mybir.AxisListType.X,
                op=ALU.min,
            )
            neg_max[unit] = minus_max

        def open_row_sums(group):
            e_sums = stats.tile([P, GROUP, HALVES], F32)
            nc.gpsimd.memset(e_sums[:], 0.0)
            row_sums[group] = e_sums

        def exponentials(unit):
            group, member = divmod(unit, GROUP)
            e_bf16 = units.tile([P, S], BF16)
            if by_tensor(unit):
                pieces = [scores[unit, half][:] for half in range(HALVES)]
            else:
                pieces = [masked[unit][:]]
            width = S // len(pieces)
            for half, score_keys in enumerate(pieces):
                nc.scalar.activation(
                    out=e_bf16[:, half * width : (half + 1) * width].rearrange(
                        "p (u x j) -> p u x j", u=PAIR, j=PAIR
                    ),
                    in_=score_keys.rearrange("p (x u j) -> p u x j", u=PAIR, j=PAIR),
                    func=ACT.Exp,
                    bias=neg_max[unit][:],
                    scale=1.0,
                    accum_out=row_sums[group][:, member, half : half + 1],
                )
            e_rows[unit] = e_bf16

        def transpose_e(unit):
            e_words = e_rows[unit][:].bitcast(F32)
            if unit < UNITS - 2:
                e_words_t = e_psum.tile([P, PASSES, PAIR, P], F32, tag="e_bank")
            else:
                e_words_t = tensor_psum.tile([P, PASSES, PAIR, P], F32, tag="tensor_bank")
            for u in range(PAIR):
                for g in range(PASSES):
                    first = (g * PAIR + u if by_tensor(unit) else u * PASSES + g) * P
                    nc.tensor.transpose(
                        e_words_t[:, g, u, :], e_words[:, first : first + P], ident_f32[:]
                    )
            e_t[unit] = e_words_t

        def regroup_e(unit, by_vector=False):
            group, member = divmod(unit, GROUP)
            if group not in e_grouped:
                grouped = groups.tile([P, GROUP, PASSES, P, PACK], BF16, align_bytes=64)
                e_grouped[group] = grouped
            (nc.vector.tensor_copy if by_vector else nc.scalar.copy)(
                out=e_grouped[group][:, member].bitcast(F32),
                in_=e_t[unit][:].rearrange("p g u n -> p g n u"),
            )

        def quantise_e(group, first=0, count=GROUP):
            if first == 0:
                codes = groups.tile([P, GROUP, PASSES, P], U32, align_bytes=64, name="e_code_words")
                scale_plane = groups.tile(
                    [P, GROUP, PASSES, P], U8, align_bytes=64, name="e_scale_plane"
                )
                e_codes[group], e_scales[group] = codes, scale_plane
            members = slice(first, first + count)
            nc.vector.quantize_mx(
                out=e_codes[group][:, members].rearrange("p m g n -> p (m g n)").bitcast(FP8X4),
                scales=e_scales[group][:, members].rearrange("p m g n -> p (m g n)"),
                in_=e_grouped[group][:, members].rearrange("p m g n t -> p (m g n t)"),
            )

        def multiply_e_v(group, first=0, count=GROUP):
            head = group * GROUP // TILES
            codes, scale_plane = e_codes[group], e_scales[group]
            if first == 0:
                pv_bank = spare_psum.tile([P, GROUP, D], F32, tag="spare_bank")
                pv[group] = pv_bank
            for member in range(first, first + count):
                for g in range(PASSES):
                    nc.tensor.matmul_mx(
                        out=pv[group][:, member, :],
                        lhsT=codes[:, member, g, :].bitcast(FP8X4),
                        lhsT_scale=scale_plane[:, member, g, :],
                        rhs=v_codes[head][:, g, :].bitcast(FP8X4),
                        rhs_scale=v_scales[head][:, g, :],
                        start=(g == 0),
                        stop=(g == PASSES - 1),
                    )

        def add_row_sums(group):
            row_totals = stats.tile([P, GROUP], F32)
            nc.gpsimd.tensor_tensor(
                out=row_totals[:],
                in0=row_sums[group][:, :, 0],
                in1=row_sums[group][:, :, 1],
                op=ALU.add,
            )
            sums[group] = row_totals

        def invert(group):
            inverse = stats.tile([P, GROUP], F32)
            nc.vector.reciprocal(out=inverse[:], in_=sums[group][:])
            row_sums[group] = inverse

        def divide_and_store(group, first=0, count=GROUP):
            head, first_tile = divmod(group * GROUP + first, TILES)
            out_sb = groups.tile([P, count, D], F32, tag="out_sb" if count == GROUP else "out_part")
            nc.vector.tensor_tensor(
                out=out_sb[:],
                in0=pv[group][:, first : first + count],
                in1=row_sums[group][:, first : first + count].unsqueeze(2).to_broadcast([P, count, D]),
                op=ALU.mult,
            )
            nc.sync.dma_start(
                out=out_heads[head][:, first_tile : first_tile + count, :], in_=out_sb[:]
            )

        PAIRS = UNITS // 2
        PAIRS_A_HEAD = TILES // 2

        def at(pair, member, stage, *args):
            if 0 <= pair < PAIRS:
                stage(2 * pair + member, *args)

        ctx.enter_context(tc.manual_schedule())
        load_first_head()
        for tile in (0, 3, 1, 2, 5):
            load_mask(tile)
        load_v(0)
        load_mask(7)
        load_head(1)
        load_mask(4)
        load_mask(6)
        load_v(1)
        open_row_sums(0)
        transpose_first_head()

        for j in range(-2, PAIRS):
            head, place = divmod(j, PAIRS_A_HEAD)
            odd_cycle = j % 2 == 1
            by_t = 0 <= j < PAIRS and by_tensor(2 * j + 1)
            q_head = (j + 5) // 4 if j >= 3 and (j + 5) % 4 == 0 else (1 if j == 0 else None)
            k_head = (j + 3) // 4 if j >= 1 and (j + 3) % 4 == 0 else None
            q_head = q_head if q_head is not None and q_head < HEADS else None
            k_head = k_head if k_head is not None and k_head < HEADS else None

            if odd_cycle and 0 <= (j - 3) // 2 < UNITS // GROUP:
                add_row_sums((j - 3) // 2)
            at(j + 1, 0, mask_by_vector, 0)
            if 0 <= j + 1 < PAIRS and not takes_detour(2 * j + 2):
                mask_by_vector(2 * j + 2, 1)
            at(j - 2, 0, transpose_e)
            if not odd_cycle and 0 <= (j - 4) // 2 < UNITS // GROUP:
                multiply_e_v((j - 4) // 2)
            if q_head is not None:
                transpose_q(q_head)
            if k_head is not None:
                transpose_k(k_head)
            if by_t:
                half_maximum(2 * j + 1, 0)
                half_maximum(2 * j + 1, 1)
            elif 0 <= j < PAIRS:
                mask_by_vector(2 * j + 1, 0)
                mask_by_vector(2 * j + 1, 1)
            if 0 <= j + 1 < PAIRS and takes_detour(2 * j + 2):
                mask_on_detour(2 * j + 2)
            at(j + 1, 1, scores_for_tensor)
            at(j - 2, 0, regroup_e)
            if k_head is not None:
                take_k(k_head)
            if j > 0:
                row_maximum(2 * j)
            at(j + 2, 0, scores_for_vector)
            if j - 1 > 0:
                exponentials(2 * j - 2)
            at(j - 1, 1, transpose_e)
            if by_t:
                combine_half_maxima(2 * j + 1)
            elif 0 <= j < PAIRS:
                row_maximum(2 * j + 1)
            if q_head is not None:
                take_q(q_head)
            if odd_cycle and 0 <= (j - 3) // 2 < UNITS // GROUP:
                quantise_e((j - 3) // 2)
                invert((j - 3) // 2)
            if not odd_cycle and 0 <= (j - 4) // 2 < UNITS // GROUP:
                divide_and_store((j - 4) // 2)
            if place == 2 and 0 <= head < HEADS:
                quantise_v(head)
            if 0 <= j + 1 < PAIRS and by_tensor(2 * j + 3):
                mask_by_tensor(2 * j + 3)
            at(j - 1, 1, regroup_e)
            if j == PAIRS - 1:
                exponentials(2 * j)
            at(j, 1, exponentials)

            if odd_cycle and 0 < (j + 1) // 2 < UNITS // GROUP:
                open_row_sums((j + 1) // 2)
            if j == -1:
                row_maximum(0)
            if place == 0 and 0 <= head < HEADS:
                regroup_v(head)
            for index, cycle in ((1, -2), (2, -1), (3, -1), (0, 0)):
                if j == cycle:
                    make_tables(index)
                    if index == 2:
                        exponentials(0)
            if place == 0 and 0 <= head < HEADS - 2:
                load_head(head + 2)
                load_v(head + 2)

        last = UNITS // GROUP - 1
        transpose_e(UNITS - 4)
        multiply_e_v(last - 1)
        transpose_e(UNITS - 2)
        regroup_e(UNITS - 4, by_vector=True)
        regroup_e(UNITS - 2)
        divide_and_store(last - 1)
        quantise_e(last, 0, 2)
        transpose_e(UNITS - 1)
        regroup_e(UNITS - 1)
        add_row_sums(last)
        invert(last)
        multiply_e_v(last, 0, 2)
        quantise_e(last, 2, 1)
        multiply_e_v(last, 2, 1)
        quantise_e(last, 3, 1)
        multiply_e_v(last, 3, 1)
        divide_and_store(last, 0, 3)
        divide_and_store(last, 3, 1)
